import numpy as np
import ml_dtypes


def mxq(x, axis, fmt="e4m3"):
    dtype, down = {"e4m3": (ml_dtypes.float8_e4m3fn, 7), "e5m2": (ml_dtypes.float8_e5m2, 14)}[fmt]
    v = np.moveaxis(np.asarray(x, np.float32).astype(ml_dtypes.bfloat16).astype(np.float64), axis, -1)
    blocks = v.reshape(v.shape[:-1] + (-1, 32))
    amax = np.abs(blocks).max(-1, keepdims=True)
    byte = np.maximum(np.where(amax > 0, np.frexp(amax)[1] - 1 + 127, 0) - down, 1)
    scale = np.exp2(byte - 127.0)
    codes = (blocks / scale).astype(np.float32).astype(dtype).astype(np.float64)
    return np.moveaxis((codes * scale).reshape(v.shape), -1, axis)


WIDE = False


def mx_kscale(k):
    if not WIDE:
        return np.ones(k)
    levels = np.array([10, -10, 5, -5, 0])
    a = np.random.permutation(np.resize(levels, k // 512 * 4)).reshape(k // 512, 4)
    idx = np.arange(k)
    return np.exp2(a[idx // 512, idx % 128 // 32])


BF16 = ml_dtypes.bfloat16


def bf(x):
    return np.asarray(x, np.float32).astype(BF16)


def f64(x):
    return np.asarray(x).astype(np.float64)


B, S, C, MID = 4, 512, 512, 1024
K0 = 2 * C


def gelu_tanh(v):
    return 0.5 * v * (1.0 + np.tanh(np.sqrt(2.0 / np.pi) * (v + 0.044715 * v**3)))


def setup_inputs():
    u = mx_kscale(K0)[:C]
    uu = np.concatenate([u, u])
    return {"sample_features": bf(np.random.standard_normal((B, S, C)) * u),
            "query_samples": bf(np.random.standard_normal((B, S, C)) * u),
            "pos_enc": bf(np.random.standard_normal((B, S, C)) * u),
            "W0": bf(np.random.standard_normal((K0, MID)) * 0.6 / np.sqrt(K0) / uu[:, None]),
            "b0": bf(np.random.standard_normal(MID) * 0.2),
            "W1": bf(np.random.standard_normal((MID, MID)) * 1.5 / np.sqrt(MID)),
            "b1": bf(np.random.standard_normal(MID) * 0.2)}


def reference(sample_features, query_samples, pos_enc, W0, b0, W1, b1):
    sf = f64(sample_features)
    q = f64(query_samples) + f64(pos_enc)
    x = np.concatenate([sf - q, q], axis=-1)
    h = gelu_tanh((mxq(x, 2, "e4m3") @ mxq(f64(W0), 0, "e4m3")) + f64(b0))
    return gelu_tanh((mxq(h, 2, "e4m3") @ mxq(f64(W1), 0, "e4m3")) + f64(b1))

@@ -1,0 +1,295 @@
+from contextlib import ExitStack
+
+import concourse.mybir as mybir
+from concourse.masks import make_identity
+
+F32 = mybir.dt.float32
+BF16 = mybir.dt.bfloat16
+U32 = mybir.dt.uint32
+U8 = mybir.dt.uint8
+FP8X4 = mybir.dt.float8_e4m3fn_x4
+GELU = mybir.ActivationFunctionType.Gelu_apprx_tanh
+SUB = mybir.AluOpType.subtract
+ADD = mybir.AluOpType.add
+
+P = 128
+NB = 4
+S = 512
+C = 512
+MID = 1024
+FLOPS = 2 * (NB * S) * (2 * C) * MID + 2 * (NB * S) * MID * MID
+
+MANUAL = True
+XL = 12
+LAG = 12
+OFF_G1 = 1
+OFF_A = 1
+OFF_G2 = 2
+OFF_HR = 2
+OFF_HQ = 3
+W_ENGINE = "VVVSVVSV"
+W_REGROUP_SLOT = [-13,-9.5,-4.5,-3,0.5,2.5,8,7.5]
+W_QUANT_SLOT = [-12.5,-8.5,-2.5,-1.5,6.5,7.5,9.5,10.5]
+W_PIECES = [(0, 0, 0), (0, 1, 0), (0, 0, 1), (0, 1, 1), (1, 0, 0), (1, 1, 0), (1, 0, 1), (1, 1, 1)]
+LOADS = [['w',0,0,0],['x',0,0,2],['w',0,1,0],['x',0,1,2],['x',1,0,2],['w',0,0,1],['w',0,1,1],['x',1,1,2],['w',1,0,0],['w',1,1,0],['x',2,0,1],['w',1,0,1],['w',1,1,1],['b1'],['x',3,0,1]]
+
+
+def tile_samplequerymessagepassing_pa_kernel(
+    tc, sample_features, query_samples, pos_enc, W0, b0, W1, b1, out
+):
+    nc = tc.nc
+    with ExitStack() as ctx:
+        const = ctx.enter_context(tc.tile_pool(name="const", bufs=1))
+        inp = ctx.enter_context(tc.tile_pool(name="inp", bufs=1))
+        wgp = ctx.enter_context(tc.tile_pool(name="wgp", bufs=3))
+        two = ctx.enter_context(tc.tile_pool(name="two", bufs=2))
+        three = ctx.enter_context(tc.tile_pool(name="three", bufs=3))
+        tmpp = ctx.enter_context(tc.tile_pool(name="tmpp", bufs=4))
+        outp = ctx.enter_context(tc.tile_pool(name="outp", bufs=4))
+        ps_acc = ctx.enter_context(tc.psum_pool(name="ps_acc", bufs=5))
+        ps_q = ctx.enter_context(tc.psum_pool(name="ps_q", bufs=2))
+        ps_s = ctx.enter_context(tc.psum_pool(name="ps_s", bufs=1))
+        if MANUAL:
+            ctx.enter_context(tc.manual_schedule())
+
+        warm = const.tile([P, 1], F32, name="warm")
+        nc.vector.memset(warm[:], 0.0)
+        nc.scalar.activation(out=warm[:], in_=warm[:], func=GELU)
+        ident = const.tile([P, P], BF16, name="ident")
+        make_identity(nc, ident[:])
+        brow = const.tile([P, P], BF16, name="brow")
+        nc.vector.memset(brow[:], 0.0)
+        b0c = const.tile([P, 8], F32, name="b0c")
+        b1bc = const.tile([P, MID], BF16, name="b1bc")
+
+        wraw = [const.tile([P, 2, 4, MID], BF16, name="wraw%d" % i) for i in range(2)]
+        wc = [const.tile([P, 2, MID], U32, name="wc%d" % i, align_bytes=64) for i in range(2)]
+        ws = [const.tile([P, 2, MID], U8, name="ws%d" % i, align_bytes=64) for i in range(2)]
+        wdram = [W0, W1]
+        srcs = {"qs": query_samples, "pe": pos_enc, "sf": sample_features}
+        xin = {}
+        for c in range(NB):
+            for nm in ("qs", "pe", "sf"):
+                xin[(nm, c)] = inp.tile([P, 4, C], BF16, name="%s%d" % (nm, c))
+
+        nc.sync.dma_start(out=brow[0:8, :], in_=b0.rearrange("(m p) -> m p", p=P))
+        for ld in LOADS:
+            if ld[0] == "x":
+                c, h, pieces = ld[1], ld[2], ld[3]
+                step = 4 // pieces
+                rs = slice(h * step, (h + 1) * step)
+                for nm in ("qs", "pe", "sf"):
+                    view = srcs[nm][c].rearrange("(p r) ch -> p r ch", r=4)
+                    nc.sync.dma_start(out=xin[(nm, c)][:, rs, :], in_=view[:, rs, :])
+            elif ld[0] == "w":
+                i, g, nh = ld[1], ld[2], ld[3]
+                ns = slice(nh * 512, (nh + 1) * 512)
+                view = wdram[i][g * 512 : (g + 1) * 512, ns].rearrange("(t p) n -> p t n", p=P)
+                nc.sync.dma_start(out=wraw[i][:, g, :, ns], in_=view)
+            else:
+                nc.sync.dma_start(out=b1bc[:], in_=b1.partition_broadcast(P))
+
+        pb = ps_acc.tile([P, P], BF16, name="pb", tag="acc")
+        nc.tensor.transpose(pb[:], brow[:], ident[:])
+
+        st = {}
+
+        def bias0():
+            nc.vector.tensor_copy(out=b0c[:], in_=pb[:, 0:8])
+
+        def regroup(eng, dst, src):
+            d = dst.rearrange("p (c i) t -> p c t i", i=4)
+            s = src.rearrange("p t (c i) -> p c t i", i=4)
+            if eng == "V":
+                nc.vector.tensor_copy(out=d, in_=s)
+            else:
+                nc.scalar.copy(out=d, in_=s)
+
+        def quant(codes, scales, grouped):
+            nc.vector.quantize_mx(
+                out=codes.bitcast(FP8X4), scales=scales, in_=grouped[:].rearrange("p n t -> p (n t)")
+            )
+
+        def op_wr(i, g, nh, eng):
+            ns = slice(nh * 512, (nh + 1) * 512)
+            wg = wgp.tile([P, 512, 4], BF16, name="wg", align_bytes=64)
+            st[("wg", i, g, nh)] = wg
+            regroup(eng, wg[:], wraw[i][:, g, :, ns])
+
+        def op_wq(i, g, nh):
+            ns = slice(nh * 512, (nh + 1) * 512)
+            quant(wc[i][:, g, ns], ws[i][:, g, ns], st[("wg", i, g, nh)])
+
+        def op_t(k):
+            c, j = k // 2, k % 2
+            pss = ps_s.tile([P, 8, P], BF16, name="pss")
+            st[("pss", k)] = pss
+            for i in range(2):
+                for t in range(4):
+                    nc.tensor.transpose(
+                        pss[:, 4 * i + t, :], xin[("sf", c)][:, 2 * j + i, t * P : (t + 1) * P], ident[:]
+                    )
+
+        def op_m(u):
+            c, r = u // 4, u % 4
+            psq = ps_q.tile([P, 4, P], F32, name="psq")
+            st[("psq", u)] = psq
+            for t in range(4):
+                ts = slice(t * P, (t + 1) * P)
+                nc.tensor.matmul(psq[:, t, :], lhsT=xin[("qs", c)][:, r, ts], rhs=ident[:], start=True, stop=False)
+                nc.tensor.matmul(psq[:, t, :], lhsT=xin[("pe", c)][:, r, ts], rhs=ident[:], start=False, stop=True)
+
+        def op_e(k):
+            sfT = two.tile([P, 8, P], BF16, name="sfT")
+            st[("sfT", k)] = sfT
+            nc.scalar.copy(out=sfT[:], in_=st[("pss", k)][:])
+
+        def xg(c):
+            if ("xg", c) not in st:
+                xg0 = two.tile([P, S, 4], BF16, name="xg0", align_bytes=64)
+                xg1 = two.tile([P, S, 4], BF16, name="xg1", align_bytes=64)
+                st[("xg", c)] = (xg0, xg1)
+            return st[("xg", c)]
+
+        def op_q(u):
+            c, r = u // 4, u % 4
+            nc.scalar.copy(
+                out=xg(c)[1][:, r * P : (r + 1) * P, :], in_=st[("psq", u)][:].rearrange("p t r -> p r t")
+            )
+
+        def op_d(u):
+            c, r = u // 4, u % 4
+            i = u % 2
+            nc.vector.tensor_tensor(
+                out=xg(c)[0][:, r * P : (r + 1) * P, :],
+                in0=st[("sfT", u // 2)][:, 4 * i : 4 * i + 4, :].rearrange("p t r -> p r t"),
+                in1=st[("psq", u)][:].rearrange("p t r -> p r t"),
+                op=SUB,
+            )
+
+        def op_xq(c, g):
+            if g == 0:
+                xc = two.tile([P, 2, S], U32, name="xc", align_bytes=64)
+                xs = two.tile([P, 2, S], U8, name="xs", align_bytes=64)
+                st[("xc", c)] = (xc, xs)
+            xc, xs = st[("xc", c)]
+            quant(xc[:, g, :], xs[:, g, :], xg(c)[g])
+
+        def mx_group(acc, lc, ls, rc, rs_):
+            for g in range(2):
+                nc.tensor.matmul_mx(
+                    out=acc[:],
+                    lhsT=lc[g].bitcast(FP8X4),
+                    lhsT_scale=ls[g],
+                    rhs=rc[g].bitcast(FP8X4),
+                    rhs_scale=rs_[g],
+                    start=(g == 0),
+                    stop=(g == 1),
+                )
+
+        def op_l1(i):
+            c, m = i // 8, i % 8
+            ms = slice(m * P, (m + 1) * P)
+            xc, xs = st[("xc", c)]
+            acc = ps_acc.tile([P, 512], F32, name="acc")
+            st[("a1", i)] = acc
+            mx_group(
+                acc,
+                [wc[0][:, g, ms] for g in range(2)],
+                [ws[0][:, g, ms] for g in range(2)],
+                [xc[:, g, :] for g in range(2)],
+                [xs[:, g, :] for g in range(2)],
+            )
+
+        def op_g1(i):
+            c, m = i // 8, i % 8
+            if m == 0:
+                hT = two.tile([P, 8, S], BF16, name="hT")
+                st[("hT", c)] = hT
+            nc.scalar.activation(
+                out=st[("hT", c)][:, m, :], in_=st[("a1", i)][:], func=GELU, bias=b0c[:, m : m + 1], scale=1.0
+            )
+
+        def op_hr(c, g):
+            hg = two.tile([P, S, 4], BF16, name="hg", align_bytes=64)
+            st[("hg", c, g)] = hg
+            regroup("V", hg[:], st[("hT", c)][:, 4 * g : 4 * g + 4, :])
+
+        def op_hq(c, g):
+            if g == 0:
+                hc = three.tile([P, 2, S], U32, name="hc", align_bytes=64)
+                hs = three.tile([P, 2, S], U8, name="hs", align_bytes=64)
+                st[("hc", c)] = (hc, hs)
+            hc, hs = st[("hc", c)]
+            quant(hc[:, g, :], hs[:, g, :], st[("hg", c, g)])
+
+        def op_l2(i):
+            c, r, n2 = i // 8, (i % 8) // 2, i % 2
+            rs = slice(r * P, (r + 1) * P)
+            ns = slice(n2 * 512, (n2 + 1) * 512)
+            hc, hs = st[("hc", c)]
+            acc = ps_acc.tile([P, 512], F32, name="acc")
+            st[("a2", i)] = acc
+            mx_group(
+                acc,
+                [hc[:, g, rs] for g in range(2)],
+                [hs[:, g, rs] for g in range(2)],
+                [wc[1][:, g, ns] for g in range(2)],
+                [ws[1][:, g, ns] for g in range(2)],
+            )
+
+        def op_a(i):
+            n2 = i % 2
+            tmp = tmpp.tile([P, 512], F32, name="tmp")
+            st[("tmp", i)] = tmp
+            nc.vector.tensor_tensor(
+                out=tmp[:], in0=st[("a2", i)][:], in1=b1bc[:, n2 * 512 : (n2 + 1) * 512], op=ADD
+            )
+
+        def op_g2(i):
+            c, r, n2 = i // 8, (i % 8) // 2, i % 2
+            if n2 == 0:
+                o = outp.tile([P, MID], F32, name="o")
+                st[("o", i // 2)] = o
+            o = st[("o", i // 2)]
+            nc.scalar.activation(out=o[:, n2 * 512 : (n2 + 1) * 512], in_=st[("tmp", i)][:], func=GELU)
+            if n2 == 1:
+                nc.sync.dma_start(out=out[c].rearrange("(p r) n -> p r n", r=4)[:, r, :], in_=o[:])
+
+        slots = {}
+
+        def put(s, fn, *a):
+            slots[s] = slots.get(s, []) + [(fn, a)]
+
+        put(-5.25, bias0)
+        for k in range(8):
+            b = 4 * k - XL
+            put(b + 0, op_t, k)
+            put(b + 1, op_m, 2 * k)
+            put(b + 3, op_m, 2 * k + 1)
+            put(b + 1, op_e, k)
+            put(b + 2, op_q, 2 * k)
+            put(b + 4, op_q, 2 * k + 1)
+            put(b + 3, op_d, 2 * k)
+            put(b + 5, op_d, 2 * k + 1)
+            if k % 2 == 1:
+                put(b + 6, op_xq, k // 2, 0)
+                put(b + 6, op_xq, k // 2, 1)
+        for i in range(32):
+            put(i, op_l1, i)
+            put(i + OFF_G1, op_g1, i)
+            put(i + LAG, op_l2, i)
+            put(i + LAG + OFF_A, op_a, i)
+            put(i + LAG + OFF_G2, op_g2, i)
+        for c in range(NB):
+            for g in range(2):
+                e = 8 * c + 4 * g + 3
+                put(e + OFF_HR, op_hr, c, g)
+                put(e + OFF_HQ, op_hq, c, g)
+        for k, (i, g, nh) in enumerate(W_PIECES):
+            put(W_REGROUP_SLOT[k], op_wr, i, g, nh, W_ENGINE[k])
+            put(W_QUANT_SLOT[k], op_wq, i, g, nh)
+
+        for s in sorted(slots):
+            for fn, a in slots[s]:
+                fn(*a)

@@ -21,12 +21,12 @@ FLOPS = 2 * (NB * S) * (2 * C) * MID + 2 * (NB * S) * MID * MID
 
 MANUAL = True
 XL = 12
-LAG = 12
+LAG = 15
 OFF_G1 = 1
 OFF_A = 1
-OFF_G2 = 2
+OFF_G2 = 3
 OFF_HR = 2
-OFF_HQ = 3
+OFF_HQ = 4
 W_ENGINE = "VVVSVVSV"
 W_REGROUP_SLOT = [-13,-9.5,-4.5,-3,0.5,2.5,8,7.5]
 W_QUANT_SLOT = [-12.5,-8.5,-2.5,-1.5,6.5,7.5,9.5,10.5]
@@ -62,7 +62,9 @@ def tile_samplequerymessagepassing_pa_kernel(
         b0c = const.tile([P, 8], F32, name="b0c")
         b1bc = const.tile([P, MID], BF16, name="b1bc")
 
-        wraw = [const.tile([P, 2, 4, MID], BF16, name="wraw%d" % i) for i in range(2)]
+        wraw = {}
+        for i, g, nh in W_PIECES:
+            wraw[(i, g, nh)] = const.tile([P, 4, 512], BF16, name="wraw%d%d%d" % (i, g, nh))
         wc = [const.tile([P, 2, MID], U32, name="wc%d" % i, align_bytes=64) for i in range(2)]
         ws = [const.tile([P, 2, MID], U8, name="ws%d" % i, align_bytes=64) for i in range(2)]
         wdram = [W0, W1]
@@ -85,7 +87,7 @@ def tile_samplequerymessagepassing_pa_kernel(
                 i, g, nh = ld[1], ld[2], ld[3]
                 ns = slice(nh * 512, (nh + 1) * 512)
                 view = wdram[i][g * 512 : (g + 1) * 512, ns].rearrange("(t p) n -> p t n", p=P)
-                nc.sync.dma_start(out=wraw[i][:, g, :, ns], in_=view)
+                nc.sync.dma_start(out=wraw[(i, g, nh)][:], in_=view)
             else:
                 nc.sync.dma_start(out=b1bc[:], in_=b1.partition_broadcast(P))
 
@@ -114,7 +116,7 @@ def tile_samplequerymessagepassing_pa_kernel(
             ns = slice(nh * 512, (nh + 1) * 512)
             wg = wgp.tile([P, 512, 4], BF16, name="wg", align_bytes=64)
             st[("wg", i, g, nh)] = wg
-            regroup(eng, wg[:], wraw[i][:, g, :, ns])
+            regroup(eng, wg[:], wraw[(i, g, nh)][:])
 
         def op_wq(i, g, nh):
             ns = slice(nh * 512, (nh + 1) * 512)
@@ -253,8 +255,12 @@ def tile_samplequerymessagepassing_pa_kernel(
                 st[("o", i // 2)] = o
             o = st[("o", i // 2)]
             nc.scalar.activation(out=o[:, n2 * 512 : (n2 + 1) * 512], in_=st[("tmp", i)][:], func=GELU)
-            if n2 == 1:
-                nc.sync.dma_start(out=out[c].rearrange("(p r) n -> p r n", r=4)[:, r, :], in_=o[:])
+            oview = out[c].rearrange("(p r) n -> p r n", r=4)
+            if i >= 30:
+                ns = slice(n2 * 512, (n2 + 1) * 512)
+                nc.sync.dma_start(out=oview[:, r, ns], in_=o[:, ns])
+            elif n2 == 1:
+                nc.sync.dma_start(out=oview[:, r, :], in_=o[:])
 
         slots = {}
 

@@ -5,6 +5,7 @@ from concourse.masks import make_identity
 
 F32 = mybir.dt.float32
 BF16 = mybir.dt.bfloat16
+I32 = mybir.dt.int32
 U32 = mybir.dt.uint32
 U8 = mybir.dt.uint8
 FP8X4 = mybir.dt.float8_e4m3fn_x4
@@ -19,19 +20,22 @@ C = 512
 MID = 1024
 FLOPS = 2 * (NB * S) * (2 * C) * MID + 2 * (NB * S) * MID * MID
 
-MANUAL = True
-XL = 12
+XL = 13
 LAG = 15
+OFF_EV = 1
+OFF_XQ = 3
 OFF_G1 = 1
 OFF_A = 1
-OFF_G2 = 3
+OFF_G2 = 4
 OFF_HR = 2
 OFF_HQ = 4
-W_ENGINE = "VVVSVVSV"
-W_REGROUP_SLOT = [-13,-9.5,-4.5,-3,0.5,2.5,8,7.5]
-W_QUANT_SLOT = [-12.5,-8.5,-2.5,-1.5,6.5,7.5,9.5,10.5]
+EV_HEAD = 0
+EV_MOD = 4
+W_ENGINE = "VVVVVVVV"
+W_REGROUP_SLOT = [-14,-13,-2.5,-2,3.5,4.5,6.5,7.5]
+W_QUANT_SLOT = [-13.5,-12.5,-1.5,-1,5.5,6.5,8.5,9.5]
 W_PIECES = [(0, 0, 0), (0, 1, 0), (0, 0, 1), (0, 1, 1), (1, 0, 0), (1, 1, 0), (1, 0, 1), (1, 1, 1)]
-LOADS = [['w',0,0,0],['x',0,0,2],['w',0,1,0],['x',0,1,2],['x',1,0,2],['w',0,0,1],['w',0,1,1],['x',1,1,2],['w',1,0,0],['w',1,1,0],['x',2,0,1],['w',1,0,1],['w',1,1,1],['b1'],['x',3,0,1]]
+LOADS = [['w',0,0,0],['x',0,0,2],['w',0,1,0],['x',0,1,2],['x',1,0,2],['w',0,0,1],['w',0,1,1],['x',1,1,2]]
 
 
 def tile_samplequerymessagepassing_pa_kernel(
@@ -40,27 +44,33 @@ def tile_samplequerymessagepassing_pa_kernel(
     nc = tc.nc
     with ExitStack() as ctx:
         const = ctx.enter_context(tc.tile_pool(name="const", bufs=1))
-        inp = ctx.enter_context(tc.tile_pool(name="inp", bufs=1))
         wgp = ctx.enter_context(tc.tile_pool(name="wgp", bufs=3))
         two = ctx.enter_context(tc.tile_pool(name="two", bufs=2))
         three = ctx.enter_context(tc.tile_pool(name="three", bufs=3))
         tmpp = ctx.enter_context(tc.tile_pool(name="tmpp", bufs=4))
         outp = ctx.enter_context(tc.tile_pool(name="outp", bufs=4))
         ps_acc = ctx.enter_context(tc.psum_pool(name="ps_acc", bufs=5))
-        ps_q = ctx.enter_context(tc.psum_pool(name="ps_q", bufs=2))
-        ps_s = ctx.enter_context(tc.psum_pool(name="ps_s", bufs=1))
-        if MANUAL:
-            ctx.enter_context(tc.manual_schedule())
+        ps_x = ctx.enter_context(tc.psum_pool(name="ps_x", bufs=3))
+        ctx.enter_context(tc.manual_schedule())
 
+        xst = [const.tile([P, 4, 4, C], BF16, name="xst%d" % i) for i in range(2)]
         warm = const.tile([P, 1], F32, name="warm")
         nc.vector.memset(warm[:], 0.0)
+        brow = const.tile([P, P], BF16, name="brow")
+        nc.vector.memset(brow[:], 0.0)
+        nc.scalar.dma_start(out=brow[0:8, :], in_=b0.rearrange("(m p) -> m p", p=P))
         nc.scalar.activation(out=warm[:], in_=warm[:], func=GELU)
         ident = const.tile([P, P], BF16, name="ident")
         make_identity(nc, ident[:])
-        brow = const.tile([P, P], BF16, name="brow")
-        nc.vector.memset(brow[:], 0.0)
+        for i in range(2):
+            for a in range(4):
+                nc.vector.memset(xst[i][:, a, :, :].bitcast(I32), 0)
         b0c = const.tile([P, 8], F32, name="b0c")
         b1bc = const.tile([P, MID], BF16, name="b1bc")
+        sm = const.tile([P, 2, 32], BF16, name="sm")
+        iv = ident[:].rearrange("p (j s) -> p j s", s=4)
+        nc.vector.tensor_tensor(out=sm[:, 1, :], in0=iv[:, :, 1], in1=iv[:, :, 2], op=ADD)
+        nc.vector.tensor_tensor(out=sm[:, 0, :], in0=iv[:, :, 0], in1=sm[:, 1, :], op=SUB)
 
         wraw = {}
         for i, g, nh in W_PIECES:
@@ -68,28 +78,30 @@ def tile_samplequerymessagepassing_pa_kernel(
         wc = [const.tile([P, 2, MID], U32, name="wc%d" % i, align_bytes=64) for i in range(2)]
         ws = [const.tile([P, 2, MID], U8, name="ws%d" % i, align_bytes=64) for i in range(2)]
         wdram = [W0, W1]
-        srcs = {"qs": query_samples, "pe": pos_enc, "sf": sample_features}
-        xin = {}
-        for c in range(NB):
-            for nm in ("qs", "pe", "sf"):
-                xin[(nm, c)] = inp.tile([P, 4, C], BF16, name="%s%d" % (nm, c))
+        srcs = [sample_features, query_samples, pos_enc]
 
-        nc.sync.dma_start(out=brow[0:8, :], in_=b0.rearrange("(m p) -> m p", p=P))
+        def load_x(c, h, pieces):
+            step = 4 // pieces
+            sl = slice(h * step, (h + 1) * step)
+            for s in range(3):
+                view = srcs[s][c].rearrange("(a j r) ch -> j a (r ch)", a=4, j=32, r=4)
+                nc.sync.dma_start(
+                    out=xst[c % 2][s:P:4, sl, :, :].rearrange("p a r ch -> p a (r ch)"), in_=view[:, sl, :]
+                )
+
+        def load_w(i, g, nh):
+            ns = slice(nh * 512, (nh + 1) * 512)
+            view = wdram[i][g * 512 : (g + 1) * 512, ns].rearrange("(t p) n -> p t n", p=P)
+            nc.sync.dma_start(out=wraw[(i, g, nh)][:], in_=view)
+
+        def load_b1():
+            nc.sync.dma_start(out=b1bc[:], in_=b1.partition_broadcast(P))
+
         for ld in LOADS:
             if ld[0] == "x":
-                c, h, pieces = ld[1], ld[2], ld[3]
-                step = 4 // pieces
-                rs = slice(h * step, (h + 1) * step)
-                for nm in ("qs", "pe", "sf"):
-                    view = srcs[nm][c].rearrange("(p r) ch -> p r ch", r=4)
-                    nc.sync.dma_start(out=xin[(nm, c)][:, rs, :], in_=view[:, rs, :])
-            elif ld[0] == "w":
-                i, g, nh = ld[1], ld[2], ld[3]
-                ns = slice(nh * 512, (nh + 1) * 512)
-                view = wdram[i][g * 512 : (g + 1) * 512, ns].rearrange("(t p) n -> p t n", p=P)
-                nc.sync.dma_start(out=wraw[(i, g, nh)][:], in_=view)
+                load_x(ld[1], ld[2], ld[3])
             else:
-                nc.sync.dma_start(out=b1bc[:], in_=b1.partition_broadcast(P))
+                load_w(ld[1], ld[2], ld[3])
 
         pb = ps_acc.tile([P, P], BF16, name="pb", tag="acc")
         nc.tensor.transpose(pb[:], brow[:], ident[:])
@@ -108,66 +120,43 @@ def tile_samplequerymessagepassing_pa_kernel(
                 nc.scalar.copy(out=d, in_=s)
 
         def quant(codes, scales, grouped):
-            nc.vector.quantize_mx(
-                out=codes.bitcast(FP8X4), scales=scales, in_=grouped[:].rearrange("p n t -> p (n t)")
-            )
+            nc.vector.quantize_mx(out=codes.bitcast(FP8X4), scales=scales, in_=grouped.rearrange("p n t -> p (n t)"))
 
         def op_wr(i, g, nh, eng):
-            ns = slice(nh * 512, (nh + 1) * 512)
             wg = wgp.tile([P, 512, 4], BF16, name="wg", align_bytes=64)
             st[("wg", i, g, nh)] = wg
             regroup(eng, wg[:], wraw[(i, g, nh)][:])
 
         def op_wq(i, g, nh):
             ns = slice(nh * 512, (nh + 1) * 512)
-            quant(wc[i][:, g, ns], ws[i][:, g, ns], st[("wg", i, g, nh)])
+            quant(wc[i][:, g, ns], ws[i][:, g, ns], st[("wg", i, g, nh)][:])
 
-        def op_t(k):
-            c, j = k // 2, k % 2
-            pss = ps_s.tile([P, 8, P], BF16, name="pss")
-            st[("pss", k)] = pss
-            for i in range(2):
+        def op_x(i):
+            c, h, r = i // 8, (i % 8) // 4, i % 4
+            psx = ps_x.tile([P, 4, 2, 64], F32, name="psx")
+            st[("psx", i)] = psx
+            for al in range(2):
                 for t in range(4):
-                    nc.tensor.transpose(
-                        pss[:, 4 * i + t, :], xin[("sf", c)][:, 2 * j + i, t * P : (t + 1) * P], ident[:]
+                    nc.tensor.matmul(
+                        psx[:, t, :, 32 * al : 32 * al + 32],
+                        lhsT=xst[c % 2][:, 2 * h + al, r, t * P : (t + 1) * P],
+                        rhs=sm[:],
+                        start=True,
+                        stop=True,
                     )
 
-        def op_m(u):
-            c, r = u // 4, u % 4
-            psq = ps_q.tile([P, 4, P], F32, name="psq")
-            st[("psq", u)] = psq
-            for t in range(4):
-                ts = slice(t * P, (t + 1) * P)
-                nc.tensor.matmul(psq[:, t, :], lhsT=xin[("qs", c)][:, r, ts], rhs=ident[:], start=True, stop=False)
-                nc.tensor.matmul(psq[:, t, :], lhsT=xin[("pe", c)][:, r, ts], rhs=ident[:], start=False, stop=True)
-
-        def op_e(k):
-            sfT = two.tile([P, 8, P], BF16, name="sfT")
-            st[("sfT", k)] = sfT
-            nc.scalar.copy(out=sfT[:], in_=st[("pss", k)][:])
-
-        def xg(c):
+        def op_ev(i, eng):
+            c, h, r = i // 8, (i % 8) // 4, i % 4
             if ("xg", c) not in st:
-                xg0 = two.tile([P, S, 4], BF16, name="xg0", align_bytes=64)
-                xg1 = two.tile([P, S, 4], BF16, name="xg1", align_bytes=64)
-                st[("xg", c)] = (xg0, xg1)
-            return st[("xg", c)]
-
-        def op_q(u):
-            c, r = u // 4, u % 4
-            nc.scalar.copy(
-                out=xg(c)[1][:, r * P : (r + 1) * P, :], in_=st[("psq", u)][:].rearrange("p t r -> p r t")
-            )
-
-        def op_d(u):
-            c, r = u // 4, u % 4
-            i = u % 2
-            nc.vector.tensor_tensor(
-                out=xg(c)[0][:, r * P : (r + 1) * P, :],
-                in0=st[("sfT", u // 2)][:, 4 * i : 4 * i + 4, :].rearrange("p t r -> p r t"),
-                in1=st[("psq", u)][:].rearrange("p t r -> p r t"),
-                op=SUB,
-            )
+                xg = two.tile([P, 2, S, 4], BF16, name="xg", align_bytes=64)
+                st[("xg", c)] = xg
+            col = 128 * r + 64 * h
+            dst = st[("xg", c)][:, :, col : col + 64, :]
+            src = st[("psx", i)][:].rearrange("p t z k -> p z k t")
+            if eng == "V":
+                nc.vector.tensor_copy(out=dst, in_=src)
+            else:
+                nc.scalar.copy(out=dst, in_=src)
 
         def op_xq(c, g):
             if g == 0:
@@ -175,7 +164,7 @@ def tile_samplequerymessagepassing_pa_kernel(
                 xs = two.tile([P, 2, S], U8, name="xs", align_bytes=64)
                 st[("xc", c)] = (xc, xs)
             xc, xs = st[("xc", c)]
-            quant(xc[:, g, :], xs[:, g, :], xg(c)[g])
+            quant(xc[:, g, :], xs[:, g, :], st[("xg", c)][:, g, :, :])
 
         def mx_group(acc, lc, ls, rc, rs_):
             for g in range(2):
@@ -223,7 +212,7 @@ def tile_samplequerymessagepassing_pa_kernel(
                 hs = three.tile([P, 2, S], U8, name="hs", align_bytes=64)
                 st[("hc", c)] = (hc, hs)
             hc, hs = st[("hc", c)]
-            quant(hc[:, g, :], hs[:, g, :], st[("hg", c, g)])
+            quant(hc[:, g, :], hs[:, g, :], st[("hg", c, g)][:])
 
         def op_l2(i):
             c, r, n2 = i // 8, (i % 8) // 2, i % 2
@@ -268,19 +257,15 @@ def tile_samplequerymessagepassing_pa_kernel(
             slots[s] = slots.get(s, []) + [(fn, a)]
 
         put(-5.25, bias0)
-        for k in range(8):
-            b = 4 * k - XL
-            put(b + 0, op_t, k)
-            put(b + 1, op_m, 2 * k)
-            put(b + 3, op_m, 2 * k + 1)
-            put(b + 1, op_e, k)
-            put(b + 2, op_q, 2 * k)
-            put(b + 4, op_q, 2 * k + 1)
-            put(b + 3, op_d, 2 * k)
-            put(b + 5, op_d, 2 * k + 1)
-            if k % 2 == 1:
-                put(b + 6, op_xq, k // 2, 0)
-                put(b + 6, op_xq, k // 2, 1)
+        for i in range(32):
+            put(i - XL, op_x, i)
+            on_v = i < EV_HEAD and i % EV_MOD == EV_MOD - 1
+            put(i - XL + OFF_EV, op_ev, i, "V" if on_v else "S")
+        for c in range(NB):
+            put(8 * c + 7 - XL + OFF_XQ, op_xq, c, 0)
+            put(8 * c + 7 - XL + OFF_XQ, op_xq, c, 1)
+        put(7 - XL + 0.25, load_x, 2, 0, 1)
+        put(15 - XL + 0.25, load_x, 3, 0, 1)
         for i in range(32):
             put(i, op_l1, i)
             put(i + OFF_G1, op_g1, i)
@@ -295,6 +280,9 @@ def tile_samplequerymessagepassing_pa_kernel(
         for k, (i, g, nh) in enumerate(W_PIECES):
             put(W_REGROUP_SLOT[k], op_wr, i, g, nh, W_ENGINE[k])
             put(W_QUANT_SLOT[k], op_wq, i, g, nh)
+        for i, g, nh in W_PIECES[4:]:
+            put(7 - XL + 0.3, load_w, i, g, nh)
+        put(7 - XL + 0.3, load_b1)
 
         for s in sorted(slots):
             for fn, a in slots[s]:

@@ -10,32 +10,19 @@ U32 = mybir.dt.uint32
 U8 = mybir.dt.uint8
 FP8X4 = mybir.dt.float8_e4m3fn_x4
 GELU = mybir.ActivationFunctionType.Gelu_apprx_tanh
-SUB = mybir.AluOpType.subtract
 ADD = mybir.AluOpType.add
+SUB = mybir.AluOpType.subtract
 
 P = 128
-NB = 4
-S = 512
+CHUNKS = 4
+TOK = 512
 C = 512
 MID = 1024
-FLOPS = 2 * (NB * S) * (2 * C) * MID + 2 * (NB * S) * MID * MID
+FLOPS = 2 * (CHUNKS * TOK) * (2 * C) * MID + 2 * (CHUNKS * TOK) * MID * MID
 
-XL = 13
+GROUPS = 8 * CHUNKS
+LEAD = 11
 LAG = 15
-OFF_EV = 1
-OFF_XQ = 3
-OFF_G1 = 1
-OFF_A = 1
-OFF_G2 = 4
-OFF_HR = 2
-OFF_HQ = 4
-EV_HEAD = 0
-EV_MOD = 4
-W_ENGINE = "VVVVVVVV"
-W_REGROUP_SLOT = [-14,-13,-2.5,-2,3.5,4.5,6.5,7.5]
-W_QUANT_SLOT = [-13.5,-12.5,-1.5,-1,5.5,6.5,8.5,9.5]
-W_PIECES = [(0, 0, 0), (0, 1, 0), (0, 0, 1), (0, 1, 1), (1, 0, 0), (1, 1, 0), (1, 0, 1), (1, 1, 1)]
-LOADS = [['w',0,0,0],['x',0,0,2],['w',0,1,0],['x',0,1,2],['x',1,0,2],['w',0,0,1],['w',0,1,1],['x',1,1,2]]
 
 
 def tile_samplequerymessagepassing_pa_kernel(
@@ -44,246 +31,240 @@ def tile_samplequerymessagepassing_pa_kernel(
     nc = tc.nc
     with ExitStack() as ctx:
         const = ctx.enter_context(tc.tile_pool(name="const", bufs=1))
-        wgp = ctx.enter_context(tc.tile_pool(name="wgp", bufs=3))
         two = ctx.enter_context(tc.tile_pool(name="two", bufs=2))
         three = ctx.enter_context(tc.tile_pool(name="three", bufs=3))
-        tmpp = ctx.enter_context(tc.tile_pool(name="tmpp", bufs=4))
-        outp = ctx.enter_context(tc.tile_pool(name="outp", bufs=4))
+        four = ctx.enter_context(tc.tile_pool(name="four", bufs=4))
         ps_acc = ctx.enter_context(tc.psum_pool(name="ps_acc", bufs=5))
         ps_x = ctx.enter_context(tc.psum_pool(name="ps_x", bufs=3))
         ctx.enter_context(tc.manual_schedule())
 
-        xst = [const.tile([P, 4, 4, C], BF16, name="xst%d" % i) for i in range(2)]
-        warm = const.tile([P, 1], F32, name="warm")
-        nc.vector.memset(warm[:], 0.0)
+        zero = const.tile([P, 1], F32, name="zero")
+        nc.vector.memset(zero[:], 0.0)
         brow = const.tile([P, P], BF16, name="brow")
         nc.vector.memset(brow[:], 0.0)
         nc.scalar.dma_start(out=brow[0:8, :], in_=b0.rearrange("(m p) -> m p", p=P))
-        nc.scalar.activation(out=warm[:], in_=warm[:], func=GELU)
+        nc.scalar.activation(out=zero[:], in_=zero[:], func=GELU)
         ident = const.tile([P, P], BF16, name="ident")
         make_identity(nc, ident[:])
-        for i in range(2):
-            for a in range(4):
-                nc.vector.memset(xst[i][:, a, :, :].bitcast(I32), 0)
-        b0c = const.tile([P, 8], F32, name="b0c")
-        b1bc = const.tile([P, MID], BF16, name="b1bc")
-        sm = const.tile([P, 2, 32], BF16, name="sm")
-        iv = ident[:].rearrange("p (j s) -> p j s", s=4)
-        nc.vector.tensor_tensor(out=sm[:, 1, :], in0=iv[:, :, 1], in1=iv[:, :, 2], op=ADD)
-        nc.vector.tensor_tensor(out=sm[:, 0, :], in0=iv[:, :, 0], in1=sm[:, 1, :], op=SUB)
+        sel = const.tile([P, 2, 32], BF16, name="sel")
+        by_slot = ident[:].rearrange("p (j s) -> p j s", s=4)
+        nc.gpsimd.tensor_tensor(out=sel[:, 1, :], in0=by_slot[:, :, 1], in1=by_slot[:, :, 2], op=ADD)
+        nc.gpsimd.tensor_tensor(out=sel[:, 0, :], in0=by_slot[:, :, 0], in1=sel[:, 1, :], op=SUB)
+        stacked = [const.tile([P, 2, 4, 2, C], BF16, name="stacked%d" % i) for i in range(2)]
+        for h in range(2):
+            nc.vector.memset(stacked[0][:, h, :, :, :].bitcast(I32), 0)
+            nc.scalar.copy(
+                out=stacked[1][:, h, :, :, :].rearrange("p a r ch -> p (a r ch)").bitcast(F32),
+                in_=zero[:].to_broadcast([P, 4 * C]),
+            )
+        b0_col = const.tile([P, 8], F32, name="b0_col")
+        b1_all = const.tile([P, MID], BF16, name="b1_all")
 
-        wraw = {}
-        for i, g, nh in W_PIECES:
-            wraw[(i, g, nh)] = const.tile([P, 4, 512], BF16, name="wraw%d%d%d" % (i, g, nh))
-        wc = [const.tile([P, 2, MID], U32, name="wc%d" % i, align_bytes=64) for i in range(2)]
-        ws = [const.tile([P, 2, MID], U8, name="ws%d" % i, align_bytes=64) for i in range(2)]
-        wdram = [W0, W1]
-        srcs = [sample_features, query_samples, pos_enc]
+        w_dram = [W0, W1]
+        w_raw = {}
+        for layer in range(2):
+            for nh in range(2):
+                for g in range(2):
+                    w_raw[(layer, g, nh)] = const.tile([P, 4, 512], BF16, name="w_raw%d%d%d" % (layer, g, nh))
+        w_codes = [const.tile([P, 2, MID], U32, name="w_codes%d" % i, align_bytes=64) for i in range(2)]
+        w_scales = [const.tile([P, 2, MID], U8, name="w_scales%d" % i, align_bytes=64) for i in range(2)]
+        live = {}
 
-        def load_x(c, h, pieces):
-            step = 4 // pieces
-            sl = slice(h * step, (h + 1) * step)
-            for s in range(3):
-                view = srcs[s][c].rearrange("(a j r) ch -> j a (r ch)", a=4, j=32, r=4)
+        def load_x(c, h):
+            for s, src in enumerate((sample_features, query_samples, pos_enc)):
+                view = src[c].rearrange("(a j h r) ch -> j h a (r ch)", a=4, j=32, h=2, r=2)
                 nc.sync.dma_start(
-                    out=xst[c % 2][s:P:4, sl, :, :].rearrange("p a r ch -> p a (r ch)"), in_=view[:, sl, :]
+                    out=stacked[c % 2][s:P:4, h, :, :, :].rearrange("p a r ch -> p a (r ch)"), in_=view[:, h, :, :]
                 )
 
-        def load_w(i, g, nh):
-            ns = slice(nh * 512, (nh + 1) * 512)
-            view = wdram[i][g * 512 : (g + 1) * 512, ns].rearrange("(t p) n -> p t n", p=P)
-            nc.sync.dma_start(out=wraw[(i, g, nh)][:], in_=view)
+        def load_w(layer, g, nh):
+            rows = w_dram[layer][g * 512 : (g + 1) * 512, nh * 512 : (nh + 1) * 512]
+            nc.sync.dma_start(out=w_raw[(layer, g, nh)][:], in_=rows.rearrange("(t p) n -> p t n", p=P))
 
-        def load_b1():
-            nc.sync.dma_start(out=b1bc[:], in_=b1.partition_broadcast(P))
+        load_w(0, 0, 0)
+        load_x(0, 0)
+        load_w(0, 1, 0)
+        load_x(0, 1)
+        load_x(1, 0)
+        load_w(0, 0, 1)
+        load_w(0, 1, 1)
+        load_x(1, 1)
+        load_w(1, 0, 0)
+        load_w(1, 1, 0)
 
-        for ld in LOADS:
-            if ld[0] == "x":
-                load_x(ld[1], ld[2], ld[3])
-            else:
-                load_w(ld[1], ld[2], ld[3])
+        def late_loads(unit):
+            if unit == 7:
+                load_x(2, 0)
+                load_x(2, 1)
+                load_w(1, 0, 1)
+                load_w(1, 1, 1)
+                nc.sync.dma_start(out=b1_all[:], in_=b1.partition_broadcast(P))
+            if unit == 15:
+                load_x(3, 0)
+                load_x(3, 1)
 
-        pb = ps_acc.tile([P, P], BF16, name="pb", tag="acc")
-        nc.tensor.transpose(pb[:], brow[:], ident[:])
+        bias_ps = ps_acc.tile([P, P], BF16, name="bias_ps", tag="acc")
+        nc.tensor.transpose(bias_ps[:], brow[:], ident[:])
 
-        st = {}
+        def regroup(dst, src):
+            nc.vector.tensor_copy(
+                out=dst.rearrange("p (c i) t -> p c t i", i=4), in_=src.rearrange("p t (c i) -> p c t i", i=4)
+            )
 
-        def bias0():
-            nc.vector.tensor_copy(out=b0c[:], in_=pb[:, 0:8])
-
-        def regroup(eng, dst, src):
-            d = dst.rearrange("p (c i) t -> p c t i", i=4)
-            s = src.rearrange("p t (c i) -> p c t i", i=4)
-            if eng == "V":
-                nc.vector.tensor_copy(out=d, in_=s)
-            else:
-                nc.scalar.copy(out=d, in_=s)
-
-        def quant(codes, scales, grouped):
+        def quantise(codes, scales, grouped):
             nc.vector.quantize_mx(out=codes.bitcast(FP8X4), scales=scales, in_=grouped.rearrange("p n t -> p (n t)"))
 
-        def op_wr(i, g, nh, eng):
-            wg = wgp.tile([P, 512, 4], BF16, name="wg", align_bytes=64)
-            st[("wg", i, g, nh)] = wg
-            regroup(eng, wg[:], wraw[(i, g, nh)][:])
+        def w_regroup(k):
+            if 0 <= k < 8:
+                key = (k // 4, k % 2, (k % 4) // 2)
+                grouped = three.tile([P, 512, 4], BF16, name="w_grouped", align_bytes=64)
+                live[("wg", k)] = grouped
+                regroup(grouped[:], w_raw[key][:])
 
-        def op_wq(i, g, nh):
-            ns = slice(nh * 512, (nh + 1) * 512)
-            quant(wc[i][:, g, ns], ws[i][:, g, ns], st[("wg", i, g, nh)][:])
+        def w_quantise(k):
+            if 0 <= k < 8:
+                layer, g, nh = k // 4, k % 2, (k % 4) // 2
+                cols = slice(nh * 512, (nh + 1) * 512)
+                quantise(w_codes[layer][:, g, cols], w_scales[layer][:, g, cols], live[("wg", k)][:])
 
-        def op_x(i):
-            c, h, r = i // 8, (i % 8) // 4, i % 4
-            psx = ps_x.tile([P, 4, 2, 64], F32, name="psx")
-            st[("psx", i)] = psx
-            for al in range(2):
-                for t in range(4):
-                    nc.tensor.matmul(
-                        psx[:, t, :, 32 * al : 32 * al + 32],
-                        lhsT=xst[c % 2][:, 2 * h + al, r, t * P : (t + 1) * P],
-                        rhs=sm[:],
-                        start=True,
-                        stop=True,
-                    )
+        def x_matmuls(u):
+            if 0 <= u < GROUPS:
+                c, r, half = u // 8, (u % 8) // 2, u % 2
+                bank = ps_x.tile([P, 4, 2, 64], F32, name="x_bank")
+                live[("xb", u)] = bank
+                for a in range(2):
+                    for t in range(4):
+                        nc.tensor.matmul(
+                            bank[:, t, :, 32 * a : 32 * a + 32],
+                            lhsT=stacked[c % 2][:, r // 2, 2 * half + a, r % 2, t * P : (t + 1) * P],
+                            rhs=sel[:],
+                            start=True,
+                            stop=True,
+                        )
+                late_loads(u)
 
-        def op_ev(i, eng):
-            c, h, r = i // 8, (i % 8) // 4, i % 4
-            if ("xg", c) not in st:
-                xg = two.tile([P, 2, S, 4], BF16, name="xg", align_bytes=64)
-                st[("xg", c)] = xg
-            col = 128 * r + 64 * h
-            dst = st[("xg", c)][:, :, col : col + 64, :]
-            src = st[("psx", i)][:].rearrange("p t z k -> p z k t")
-            if eng == "V":
-                nc.vector.tensor_copy(out=dst, in_=src)
-            else:
-                nc.scalar.copy(out=dst, in_=src)
+        def x_copy(u):
+            if 0 <= u < GROUPS:
+                c, r, half = u // 8, (u % 8) // 2, u % 2
+                if u % 8 == 0:
+                    x_grouped = two.tile([P, 2, TOK, 4], BF16, name="x_grouped", align_bytes=64)
+                    live[("xg", c)] = x_grouped
+                col = 128 * r + 64 * half
+                dst = live[("xg", c)][:, :, col : col + 64, :]
+                src = live[("xb", u)][:].rearrange("p t z k -> p z k t")
+                if u < 8 and u % 2 == 1:
+                    nc.vector.tensor_copy(out=dst, in_=src)
+                else:
+                    nc.scalar.copy(out=dst, in_=src)
 
-        def op_xq(c, g):
-            if g == 0:
-                xc = two.tile([P, 2, S], U32, name="xc", align_bytes=64)
-                xs = two.tile([P, 2, S], U8, name="xs", align_bytes=64)
-                st[("xc", c)] = (xc, xs)
-            xc, xs = st[("xc", c)]
-            quant(xc[:, g, :], xs[:, g, :], st[("xg", c)][:, g, :, :])
+        def x_quantise(u):
+            if 0 <= u < GROUPS and u % 8 == 7:
+                c = u // 8
+                codes = two.tile([P, 2, TOK], U32, name="x_codes", align_bytes=64)
+                scales = two.tile([P, 2, TOK], U8, name="x_scales", align_bytes=64)
+                live[("xq", c)] = (codes, scales)
+                for z in range(2):
+                    quantise(codes[:, z, :], scales[:, z, :], live[("xg", c)][:, z, :, :])
 
-        def mx_group(acc, lc, ls, rc, rs_):
+        def mx_group(key, lhs, lhs_cols, rhs, rhs_cols):
+            acc = ps_acc.tile([P, 512], F32, name="acc")
+            live[key] = acc
             for g in range(2):
                 nc.tensor.matmul_mx(
                     out=acc[:],
-                    lhsT=lc[g].bitcast(FP8X4),
-                    lhsT_scale=ls[g],
-                    rhs=rc[g].bitcast(FP8X4),
-                    rhs_scale=rs_[g],
+                    lhsT=lhs[0][:, g, lhs_cols].bitcast(FP8X4),
+                    lhsT_scale=lhs[1][:, g, lhs_cols],
+                    rhs=rhs[0][:, g, rhs_cols].bitcast(FP8X4),
+                    rhs_scale=rhs[1][:, g, rhs_cols],
                     start=(g == 0),
                     stop=(g == 1),
                 )
 
-        def op_l1(i):
-            c, m = i // 8, i % 8
-            ms = slice(m * P, (m + 1) * P)
-            xc, xs = st[("xc", c)]
-            acc = ps_acc.tile([P, 512], F32, name="acc")
-            st[("a1", i)] = acc
-            mx_group(
-                acc,
-                [wc[0][:, g, ms] for g in range(2)],
-                [ws[0][:, g, ms] for g in range(2)],
-                [xc[:, g, :] for g in range(2)],
-                [xs[:, g, :] for g in range(2)],
-            )
+        def layer1(i):
+            if 0 <= i < GROUPS:
+                c, m = i // 8, i % 8
+                mx_group(("a1", i), (w_codes[0], w_scales[0]), slice(m * P, (m + 1) * P), live[("xq", c)], slice(0, TOK))
 
-        def op_g1(i):
-            c, m = i // 8, i % 8
-            if m == 0:
-                hT = two.tile([P, 8, S], BF16, name="hT")
-                st[("hT", c)] = hT
-            nc.scalar.activation(
-                out=st[("hT", c)][:, m, :], in_=st[("a1", i)][:], func=GELU, bias=b0c[:, m : m + 1], scale=1.0
-            )
+        def gelu1(i):
+            if 0 <= i < GROUPS:
+                c, m = i // 8, i % 8
+                if m == 0:
+                    h_t = two.tile([P, 8, TOK], BF16, name="h_t")
+                    live[("hT", c)] = h_t
+                nc.scalar.activation(
+                    out=live[("hT", c)][:, m, :], in_=live[("a1", i)][:], func=GELU, bias=b0_col[:, m : m + 1], scale=1.0
+                )
 
-        def op_hr(c, g):
-            hg = two.tile([P, S, 4], BF16, name="hg", align_bytes=64)
-            st[("hg", c, g)] = hg
-            regroup("V", hg[:], st[("hT", c)][:, 4 * g : 4 * g + 4, :])
+        def h_regroup(i):
+            if 0 <= i < GROUPS and i % 4 == 3:
+                c, g = i // 8, (i % 8) // 4
+                grouped = two.tile([P, TOK, 4], BF16, name="h_grouped", align_bytes=64)
+                live[("hg", c, g)] = grouped
+                regroup(grouped[:], live[("hT", c)][:, 4 * g : 4 * g + 4, :])
 
-        def op_hq(c, g):
-            if g == 0:
-                hc = three.tile([P, 2, S], U32, name="hc", align_bytes=64)
-                hs = three.tile([P, 2, S], U8, name="hs", align_bytes=64)
-                st[("hc", c)] = (hc, hs)
-            hc, hs = st[("hc", c)]
-            quant(hc[:, g, :], hs[:, g, :], st[("hg", c, g)][:])
+        def h_quantise(i):
+            if 0 <= i < GROUPS and i % 4 == 3:
+                c, g = i // 8, (i % 8) // 4
+                if g == 0:
+                    codes = three.tile([P, 2, TOK], U32, name="h_codes", align_bytes=64)
+                    scales = three.tile([P, 2, TOK], U8, name="h_scales", align_bytes=64)
+                    live[("hq", c)] = (codes, scales)
+                codes, scales = live[("hq", c)]
+                quantise(codes[:, g, :], scales[:, g, :], live[("hg", c, g)][:])
 
-        def op_l2(i):
-            c, r, n2 = i // 8, (i % 8) // 2, i % 2
-            rs = slice(r * P, (r + 1) * P)
-            ns = slice(n2 * 512, (n2 + 1) * 512)
-            hc, hs = st[("hc", c)]
-            acc = ps_acc.tile([P, 512], F32, name="acc")
-            st[("a2", i)] = acc
-            mx_group(
-                acc,
-                [hc[:, g, rs] for g in range(2)],
-                [hs[:, g, rs] for g in range(2)],
-                [wc[1][:, g, ns] for g in range(2)],
-                [ws[1][:, g, ns] for g in range(2)],
-            )
+        def layer2(i):
+            if 0 <= i < GROUPS:
+                c, r, nh = i // 8, (i % 8) // 2, i % 2
+                mx_group(
+                    ("a2", i), live[("hq", c)], slice(r * P, (r + 1) * P),
+                    (w_codes[1], w_scales[1]), slice(nh * 512, (nh + 1) * 512),
+                )
 
-        def op_a(i):
-            n2 = i % 2
-            tmp = tmpp.tile([P, 512], F32, name="tmp")
-            st[("tmp", i)] = tmp
-            nc.vector.tensor_tensor(
-                out=tmp[:], in0=st[("a2", i)][:], in1=b1bc[:, n2 * 512 : (n2 + 1) * 512], op=ADD
-            )
+        def add_b1(i):
+            if 0 <= i < GROUPS:
+                nh = i % 2
+                biased = four.tile([P, 512], F32, name="biased")
+                live[("t", i)] = biased
+                nc.vector.tensor_tensor(
+                    out=biased[:], in0=live[("a2", i)][:], in1=b1_all[:, nh * 512 : (nh + 1) * 512], op=ADD
+                )
 
-        def op_g2(i):
-            c, r, n2 = i // 8, (i % 8) // 2, i % 2
-            if n2 == 0:
-                o = outp.tile([P, MID], F32, name="o")
-                st[("o", i // 2)] = o
-            o = st[("o", i // 2)]
-            nc.scalar.activation(out=o[:, n2 * 512 : (n2 + 1) * 512], in_=st[("tmp", i)][:], func=GELU)
-            oview = out[c].rearrange("(p r) n -> p r n", r=4)
-            if i >= 30:
-                ns = slice(n2 * 512, (n2 + 1) * 512)
-                nc.sync.dma_start(out=oview[:, r, ns], in_=o[:, ns])
-            elif n2 == 1:
-                nc.sync.dma_start(out=oview[:, r, :], in_=o[:])
+        def gelu2_store(i):
+            if 0 <= i < GROUPS:
+                c, r, nh = i // 8, (i % 8) // 2, i % 2
+                if nh == 0:
+                    rows = four.tile([P, MID], F32, name="rows")
+                    live[("o", i // 2)] = rows
+                rows = live[("o", i // 2)]
+                cols = slice(nh * 512, (nh + 1) * 512)
+                nc.scalar.activation(out=rows[:, cols], in_=live[("t", i)][:], func=GELU)
+                dram = out[c].rearrange("(p r) n -> p r n", r=4)
+                if i >= GROUPS - 2:
+                    nc.sync.dma_start(out=dram[:, r, cols], in_=rows[:, cols])
+                elif nh == 1:
+                    nc.sync.dma_start(out=dram[:, r, :], in_=rows[:])
 
-        slots = {}
+        def w_slot(k):
+            return 2 * k - 7 if k < 4 else 3 * k - 10
 
-        def put(s, fn, *a):
-            slots[s] = slots.get(s, []) + [(fn, a)]
-
-        put(-5.25, bias0)
-        for i in range(32):
-            put(i - XL, op_x, i)
-            on_v = i < EV_HEAD and i % EV_MOD == EV_MOD - 1
-            put(i - XL + OFF_EV, op_ev, i, "V" if on_v else "S")
-        for c in range(NB):
-            put(8 * c + 7 - XL + OFF_XQ, op_xq, c, 0)
-            put(8 * c + 7 - XL + OFF_XQ, op_xq, c, 1)
-        put(7 - XL + 0.25, load_x, 2, 0, 1)
-        put(15 - XL + 0.25, load_x, 3, 0, 1)
-        for i in range(32):
-            put(i, op_l1, i)
-            put(i + OFF_G1, op_g1, i)
-            put(i + LAG, op_l2, i)
-            put(i + LAG + OFF_A, op_a, i)
-            put(i + LAG + OFF_G2, op_g2, i)
-        for c in range(NB):
-            for g in range(2):
-                e = 8 * c + 4 * g + 3
-                put(e + OFF_HR, op_hr, c, g)
-                put(e + OFF_HQ, op_hq, c, g)
-        for k, (i, g, nh) in enumerate(W_PIECES):
-            put(W_REGROUP_SLOT[k], op_wr, i, g, nh, W_ENGINE[k])
-            put(W_QUANT_SLOT[k], op_wq, i, g, nh)
-        for i, g, nh in W_PIECES[4:]:
-            put(7 - XL + 0.3, load_w, i, g, nh)
-        put(7 - XL + 0.3, load_b1)
-
-        for s in sorted(slots):
-            for fn, a in slots[s]:
-                fn(*a)
+        w_regroup(0)
+        w_regroup(1)
+        w_quantise(0)
+        w_quantise(1)
+        nc.vector.tensor_copy(out=b0_col[:], in_=bias_ps[:, 0:8])
+        for s in range(-LEAD, GROUPS + LAG + 4):
+            x_matmuls(s + LEAD)
+            layer2(s - LAG)
+            layer1(s)
+            x_copy(s + LEAD - 1)
+            gelu2_store(s - LAG - 4)
+            gelu1(s - 1)
+            x_quantise(s + LEAD - 2)
+            add_b1(s - LAG - 1)
+            h_regroup(s - 2)
+            h_quantise(s - 4)
+            for k in range(2, 8):
+                if s == w_slot(k):
+                    w_regroup(k)
+                if s == w_slot(k) + 1:
+                    w_quantise(k)

@@ -50,11 +50,11 @@ def tile_samplequerymessagepassing_pa_kernel(
         by_slot = ident[:].rearrange("p (j s) -> p j s", s=4)
         nc.gpsimd.tensor_tensor(out=sel[:, 1, :], in0=by_slot[:, :, 1], in1=by_slot[:, :, 2], op=ADD)
         nc.gpsimd.tensor_tensor(out=sel[:, 0, :], in0=by_slot[:, :, 0], in1=sel[:, 1, :], op=SUB)
-        stacked = [const.tile([P, 2, 4, 2, C], BF16, name="stacked%d" % i) for i in range(2)]
+        stacked = [const.tile([P, 2, 16, C // 2], BF16, name="stacked%d" % i) for i in range(2)]
         for h in range(2):
-            nc.vector.memset(stacked[0][:, h, :, :, :].bitcast(I32), 0)
+            nc.vector.memset(stacked[0][:, h, :, :].bitcast(I32), 0)
             nc.scalar.copy(
-                out=stacked[1][:, h, :, :, :].rearrange("p a r ch -> p (a r ch)").bitcast(F32),
+                out=stacked[1][:, h, :, :].rearrange("p g ch -> p (g ch)").bitcast(F32),
                 in_=zero[:].to_broadcast([P, 4 * C]),
             )
         b0_col = const.tile([P, 8], F32, name="b0_col")
@@ -72,14 +72,18 @@ def tile_samplequerymessagepassing_pa_kernel(
 
         def load_x(c, h):
             for s, src in enumerate((sample_features, query_samples, pos_enc)):
-                view = src[c].rearrange("(a j h r) ch -> j h a (r ch)", a=4, j=32, h=2, r=2)
-                nc.sync.dma_start(
-                    out=stacked[c % 2][s:P:4, h, :, :, :].rearrange("p a r ch -> p a (r ch)"), in_=view[:, h, :, :]
-                )
+                view = src[c].rearrange("(h g j) (u ch) -> (j u) h g ch", h=2, g=16, u=2)
+                nc.sync.dma_start(out=stacked[c % 2][s:P:4, h, :, :], in_=view[:, h, :, :])
 
         def load_w(layer, g, nh):
             rows = w_dram[layer][g * 512 : (g + 1) * 512, nh * 512 : (nh + 1) * 512]
-            nc.sync.dma_start(out=w_raw[(layer, g, nh)][:], in_=rows.rearrange("(t p) n -> p t n", p=P))
+            raw = w_raw[(layer, g, nh)]
+            if layer == 0:
+                blocks = rows.rearrange("(u v p) n -> p v u n", v=2, p=P)
+                for v in range(2):
+                    nc.sync.dma_start(out=raw[:, 2 * v : 2 * v + 2, :], in_=blocks[:, v, :, :])
+            else:
+                nc.sync.dma_start(out=raw[:], in_=rows.rearrange("(t p) n -> p t n", p=P))
 
         load_w(0, 0, 0)
         load_x(0, 0)
@@ -130,17 +134,18 @@ def tile_samplequerymessagepassing_pa_kernel(
         def x_matmuls(u):
             if 0 <= u < GROUPS:
                 c, r, half = u // 8, (u % 8) // 2, u % 2
-                bank = ps_x.tile([P, 4, 2, 64], F32, name="x_bank")
-                live[("xb", u)] = bank
-                for a in range(2):
-                    for t in range(4):
-                        nc.tensor.matmul(
-                            bank[:, t, :, 32 * a : 32 * a + 32],
-                            lhsT=stacked[c % 2][:, r // 2, 2 * half + a, r % 2, t * P : (t + 1) * P],
-                            rhs=sel[:],
-                            start=True,
-                            stop=True,
-                        )
+                if half == 0:
+                    bank = ps_x.tile([P, 2, 2, P], F32, name="x_bank")
+                    live[("xb", u // 2)] = bank
+                pairs = live[("xb", u // 2)][:].bitcast(BF16)
+                for i in range(8):
+                    nc.tensor.matmul(
+                        pairs[:, half, :, 32 * i : 32 * i + 32],
+                        lhsT=stacked[c % 2][:, r // 2, 8 * (r % 2) + i, half * P : (half + 1) * P],
+                        rhs=sel[:],
+                        start=True,
+                        stop=True,
+                    )
                 late_loads(u)
 
         def x_copy(u):
@@ -149,12 +154,9 @@ def tile_samplequerymessagepassing_pa_kernel(
                 if u % 8 == 0:
                     x_grouped = two.tile([P, 2, TOK, 4], BF16, name="x_grouped", align_bytes=64)
                     live[("xg", c)] = x_grouped
-                col = 128 * r + 64 * half
-                dst = live[("xg", c)][:, :, col : col + 64, :]
-                src = live[("xb", u)][:].rearrange("p t z k -> p z k t")
-                if u < 8 and u % 2 == 1:
-                    nc.vector.tensor_copy(out=dst, in_=src)
-                else:
+                if half == 1:
+                    dst = live[("xg", c)][:, :, 128 * r : 128 * r + 128, :].bitcast(F32)
+                    src = live[("xb", u // 2)][:].rearrange("p v z k -> p z k v")
                     nc.scalar.copy(out=dst, in_=src)
 
         def x_quantise(u):
@@ -238,14 +240,14 @@ def tile_samplequerymessagepassing_pa_kernel(
                 rows = live[("o", i // 2)]
                 cols = slice(nh * 512, (nh + 1) * 512)
                 nc.scalar.activation(out=rows[:, cols], in_=live[("t", i)][:], func=GELU)
-                dram = out[c].rearrange("(p r) n -> p r n", r=4)
+                dram = out[c].rearrange("(r p) n -> p r n", r=4)
                 if i >= GROUPS - 2:
                     nc.sync.dma_start(out=dram[:, r, cols], in_=rows[:, cols])
                 elif nh == 1:
                     nc.sync.dma_start(out=dram[:, r, :], in_=rows[:])
 
         def w_slot(k):
-            return 2 * k - 7 if k < 4 else 3 * k - 10
+            return 2 * k - 5 if k < 4 else 3 * k - 10
 
         w_regroup(0)
         w_regroup(1)

@@ -12,6 +12,7 @@ FP8X4 = mybir.dt.float8_e4m3fn_x4
 GELU = mybir.ActivationFunctionType.Gelu_apprx_tanh
 ADD = mybir.AluOpType.add
 SUB = mybir.AluOpType.subtract
+MULT = mybir.AluOpType.mult
 
 P = 128
 CHUNKS = 4
@@ -20,9 +21,14 @@ C = 512
 MID = 1024
 FLOPS = 2 * (CHUNKS * TOK) * (2 * C) * MID + 2 * (CHUNKS * TOK) * MID * MID
 
-GROUPS = 8 * CHUNKS
-LEAD = 11
-LAG = 15
+STEPS = 8 * CHUNKS
+LAG = 13
+PAIRED = [2,3]
+W_PIECES = [(0, 0, 0, 256), (0, 1, 0, 256), (0, 0, 256, 256), (0, 1, 256, 256), (0, 0, 512, 512), (0, 1, 512, 512), (1, 0, 0, 512), (1, 0, 512, 512), (1, 1, 0, 512), (1, 1, 512, 512)]
+
+
+def block(t):
+    return 2 * (t % 2) + t // 2
 
 
 def tile_samplequerymessagepassing_pa_kernel(
@@ -43,137 +49,185 @@ def tile_samplequerymessagepassing_pa_kernel(
         brow = const.tile([P, P], BF16, name="brow")
         nc.vector.memset(brow[:], 0.0)
         nc.scalar.dma_start(out=brow[0:8, :], in_=b0.rearrange("(m p) -> m p", p=P))
+        nc.scalar.dma_start(out=brow[8:16, :], in_=b1.rearrange("(m p) -> m p", p=P))
+        stacked = [[const.tile([P, 2, 4, C], BF16, name="stacked%d%d" % (i, h)) for h in range(2)] for i in range(2)]
+
+        def zero_v(t):
+            nc.vector.memset(t[:].bitcast(I32), 0)
+
+        def zero_s(t):
+            nc.scalar.copy(out=t[:].rearrange("p a r ch -> p (a r ch)").bitcast(F32), in_=zero[:].to_broadcast([P, 4 * C]))
+
+        zero_v(stacked[0][0])
+        zero_v(stacked[0][1])
         nc.scalar.activation(out=zero[:], in_=zero[:], func=GELU)
+        zero_s(stacked[1][0])
         ident = const.tile([P, P], BF16, name="ident")
         make_identity(nc, ident[:])
         sel = const.tile([P, 2, 32], BF16, name="sel")
         by_slot = ident[:].rearrange("p (j s) -> p j s", s=4)
         nc.gpsimd.tensor_tensor(out=sel[:, 1, :], in0=by_slot[:, :, 1], in1=by_slot[:, :, 2], op=ADD)
         nc.gpsimd.tensor_tensor(out=sel[:, 0, :], in0=by_slot[:, :, 0], in1=sel[:, 1, :], op=SUB)
-        stacked = [const.tile([P, 2, 16, C // 2], BF16, name="stacked%d" % i) for i in range(2)]
-        for h in range(2):
-            nc.vector.memset(stacked[0][:, h, :, :].bitcast(I32), 0)
-            nc.scalar.copy(
-                out=stacked[1][:, h, :, :].rearrange("p g ch -> p (g ch)").bitcast(F32),
-                in_=zero[:].to_broadcast([P, 4 * C]),
-            )
+        nc.gpsimd.memset(stacked[1][1][:].bitcast(I32), 0)
         b0_col = const.tile([P, 8], F32, name="b0_col")
+        b1_col = const.tile([P, 8], BF16, name="b1_col")
         b1_all = const.tile([P, MID], BF16, name="b1_all")
 
-        w_dram = [W0, W1]
-        w_raw = {}
-        for layer in range(2):
-            for nh in range(2):
-                for g in range(2):
-                    w_raw[(layer, g, nh)] = const.tile([P, 4, 512], BF16, name="w_raw%d%d%d" % (layer, g, nh))
+        w0_raw = [const.tile([P, 4, W_PIECES[k][3]], BF16, name="w0_raw%d" % k) for k in range(6)]
+        w1_raw = [const.tile([P, 4, MID], BF16, name="w1_raw%d" % g) for g in range(2)]
         w_codes = [const.tile([P, 2, MID], U32, name="w_codes%d" % i, align_bytes=64) for i in range(2)]
         w_scales = [const.tile([P, 2, MID], U8, name="w_scales%d" % i, align_bytes=64) for i in range(2)]
         live = {}
 
         def load_x(c, h):
             for s, src in enumerate((sample_features, query_samples, pos_enc)):
-                view = src[c].rearrange("(h g j) (u ch) -> (j u) h g ch", h=2, g=16, u=2)
-                nc.sync.dma_start(out=stacked[c % 2][s:P:4, h, :, :], in_=view[:, h, :, :])
+                dst = stacked[c % 2][h][s:P:4, :, :, :]
+                if c in PAIRED:
+                    view = src[c].rearrange("(h g j) (u ch) -> (j u) h g ch", h=2, g=16, u=2)
+                    nc.sync.dma_start(out=dst.rearrange("p a r (q ch) -> p (a r q) ch", q=2), in_=view[:, h, :, :])
+                else:
+                    view = src[c].rearrange("(a j r) ch -> j a (r ch)", a=4, r=4)
+                    nc.sync.dma_start(out=dst.rearrange("p a r ch -> p a (r ch)"), in_=view[:, 2 * h : 2 * h + 2, :])
 
-        def load_w(layer, g, nh):
-            rows = w_dram[layer][g * 512 : (g + 1) * 512, nh * 512 : (nh + 1) * 512]
-            raw = w_raw[(layer, g, nh)]
-            if layer == 0:
-                blocks = rows.rearrange("(u v p) n -> p v u n", v=2, p=P)
-                for v in range(2):
-                    nc.sync.dma_start(out=raw[:, 2 * v : 2 * v + 2, :], in_=blocks[:, v, :, :])
+        def load_w0(k):
+            layer, g, col, width = W_PIECES[k]
+            rows = W0[g * 512 : (g + 1) * 512, col : col + width].rearrange("(u v p) n -> p v u n", v=2, p=P)
+            for v in range(2):
+                nc.sync.dma_start(out=w0_raw[k][:, 2 * v : 2 * v + 2, :], in_=rows[:, v, :, :])
+
+        def load(name):
+            if name[0] == "w":
+                load_w0(int(name[1]))
+            elif name[0] == "v":
+                g = int(name[1])
+                nc.sync.dma_start(out=w1_raw[g][:], in_=W1[g * 512 : (g + 1) * 512, :].rearrange("(t p) n -> p t n", p=P))
             else:
-                nc.sync.dma_start(out=raw[:], in_=rows.rearrange("(t p) n -> p t n", p=P))
+                load_x(int(name[1]), int(name[2]))
 
-        load_w(0, 0, 0)
-        load_x(0, 0)
-        load_w(0, 1, 0)
-        load_x(0, 1)
-        load_x(1, 0)
-        load_w(0, 0, 1)
-        load_w(0, 1, 1)
-        load_x(1, 1)
-        load_w(1, 0, 0)
-        load_w(1, 1, 0)
-
-        def late_loads(unit):
-            if unit == 7:
-                load_x(2, 0)
-                load_x(2, 1)
-                load_w(1, 0, 1)
-                load_w(1, 1, 1)
-                nc.sync.dma_start(out=b1_all[:], in_=b1.partition_broadcast(P))
-            if unit == 15:
-                load_x(3, 0)
-                load_x(3, 1)
-
+        for name in ["w0","x00","w1","w2","w3","x01","w4","w5","x10","v0","x11","v1"]:
+            load(name)
         bias_ps = ps_acc.tile([P, P], BF16, name="bias_ps", tag="acc")
         nc.tensor.transpose(bias_ps[:], brow[:], ident[:])
+        nc.vector.tensor_copy(out=b0_col[:], in_=bias_ps[:, 0:8])
+        nc.vector.tensor_copy(out=b1_col[:], in_=bias_ps[:, 8:16])
 
-        def regroup(dst, src):
-            nc.vector.tensor_copy(
-                out=dst.rearrange("p (c i) t -> p c t i", i=4), in_=src.rearrange("p t (c i) -> p c t i", i=4)
-            )
+        def regroup(copy, dst, src):
+            copy(out=dst.rearrange("p (c i) t -> p c t i", i=4), in_=src.rearrange("p t (c i) -> p c t i", i=4))
 
         def quantise(codes, scales, grouped):
             nc.vector.quantize_mx(out=codes.bitcast(FP8X4), scales=scales, in_=grouped.rearrange("p n t -> p (n t)"))
 
+        def w_source(k):
+            layer, g, col, width = W_PIECES[k]
+            return w0_raw[k][:] if layer == 0 else w1_raw[g][:, :, col : col + width]
+
         def w_regroup(k):
-            if 0 <= k < 8:
-                key = (k // 4, k % 2, (k % 4) // 2)
-                grouped = three.tile([P, 512, 4], BF16, name="w_grouped", align_bytes=64)
-                live[("wg", k)] = grouped
-                regroup(grouped[:], w_raw[key][:])
+            width = W_PIECES[k][3]
+            grouped = three.tile([P, 512, 4], BF16, name="w_grouped", align_bytes=64)
+            live[("wg", k)] = grouped
+            src = w_source(k)
+            if k in [5,8]:
+                for n0 in range(0, width, 256):
+                    bank = ps_acc.tile([P, 512], F32, name="w_bank", tag="acc")
+                    for q in range(2):
+                        n1 = n0 + 128 * q
+                        nc.tensor.matmul(
+                            bank[:].bitcast(BF16)[:, 512 * q : 512 * q + 512],
+                            lhsT=ident[:],
+                            rhs=src[:, :, n1 : n1 + 128].rearrange("p t n -> p n t"),
+                            start=True,
+                            stop=True,
+                        )
+                    copy = nc.vector.tensor_copy if k in [] else nc.scalar.copy
+                    copy(out=grouped[:, n0 : n0 + 256, :].rearrange("p n t -> p (n t)").bitcast(F32), in_=bank[:])
+            elif k in []:
+                for n0 in range(0, width, 128):
+                    nc.gpsimd.tensor_scalar(
+                        out=grouped[:, n0 : n0 + 128, :].rearrange("p (c i) t -> p c t i", i=4),
+                        in0=src[:, :, n0 : n0 + 128].rearrange("p t (c i) -> p c t i", i=4),
+                        scalar1=1.0,
+                        scalar2=0.0,
+                        op0=MULT,
+                        op1=ADD,
+                    )
+            else:
+                regroup(nc.scalar.copy if k in [3] else nc.vector.tensor_copy, grouped[:, 0:width, :], src)
 
         def w_quantise(k):
-            if 0 <= k < 8:
-                layer, g, nh = k // 4, k % 2, (k % 4) // 2
-                cols = slice(nh * 512, (nh + 1) * 512)
-                quantise(w_codes[layer][:, g, cols], w_scales[layer][:, g, cols], live[("wg", k)][:])
+            layer, g, col, width = W_PIECES[k]
+            cols = slice(col, col + width)
+            quantise(w_codes[layer][:, g, cols], w_scales[layer][:, g, cols], live[("wg", k)][:, 0:width, :])
 
-        def x_matmuls(u):
-            if 0 <= u < GROUPS:
-                c, r, half = u // 8, (u % 8) // 2, u % 2
-                if half == 0:
-                    bank = ps_x.tile([P, 2, 2, P], F32, name="x_bank")
-                    live[("xb", u // 2)] = bank
-                pairs = live[("xb", u // 2)][:].bitcast(BF16)
-                for i in range(8):
+        def x_group(c):
+            if ("xg", c) not in live:
+                x_grouped = two.tile([P, 2, TOK, 4], BF16, name="x_grouped", align_bytes=64)
+                live[("xg", c)] = x_grouped
+            return live[("xg", c)]
+
+        def x_late(c, h):
+            if c + 2 < CHUNKS:
+                load_x(c + 2, h)
+                if (c, h) == (0, 1):
+                    for name in []:
+                        load(name)
+
+        def x_wide(u):
+            c, h, r = u // 8, (u % 8) // 4, u % 4
+            bank = ps_x.tile([P, 4, 2, 64], F32, name="x_bank")
+            for a in range(2):
+                for t in range(4):
                     nc.tensor.matmul(
-                        pairs[:, half, :, 32 * i : 32 * i + 32],
-                        lhsT=stacked[c % 2][:, r // 2, 8 * (r % 2) + i, half * P : (half + 1) * P],
+                        bank[:, t, :, 32 * a : 32 * a + 32],
+                        lhsT=stacked[c % 2][h][:, a, r, block(t) * P : (block(t) + 1) * P],
                         rhs=sel[:],
                         start=True,
                         stop=True,
                     )
-                late_loads(u)
+            col = 256 * h + 64 * r if c == 0 else 128 * r + 64 * h
+            copy = nc.vector.tensor_copy if u in [] else nc.scalar.copy
+            copy(out=x_group(c)[:, :, col : col + 64, :], in_=bank[:].rearrange("p t z k -> p z k t"))
+            if u % 4 == 3:
+                x_late(c, h)
 
-        def x_copy(u):
-            if 0 <= u < GROUPS:
-                c, r, half = u // 8, (u % 8) // 2, u % 2
-                if u % 8 == 0:
-                    x_grouped = two.tile([P, 2, TOK, 4], BF16, name="x_grouped", align_bytes=64)
-                    live[("xg", c)] = x_grouped
-                if half == 1:
-                    dst = live[("xg", c)][:, :, 128 * r : 128 * r + 128, :].bitcast(F32)
-                    src = live[("xb", u // 2)][:].rearrange("p v z k -> p z k v")
-                    nc.scalar.copy(out=dst, in_=src)
+        def x_paired(b):
+            c, r = b // 4, b % 4
+            bank = ps_x.tile([P, 2, 2, P], F32, name="x_bank")
+            pairs = bank[:].bitcast(BF16)
+            rows = stacked[c % 2][r // 2][:].rearrange("p a r (q ch) -> p (a r q) ch", q=2)
+            for v in range(2):
+                for i in range(8):
+                    nc.tensor.matmul(
+                        pairs[:, v, :, 32 * i : 32 * i + 32],
+                        lhsT=rows[:, 8 * (r % 2) + i, v * P : (v + 1) * P],
+                        rhs=sel[:],
+                        start=True,
+                        stop=True,
+                    )
+            live[("xb", b)] = bank
+            if r % 2 == 1:
+                x_late(c, r // 2)
 
-        def x_quantise(u):
-            if 0 <= u < GROUPS and u % 8 == 7:
-                c = u // 8
+        def x_paired_copy(b):
+            c, r = b // 4, b % 4
+            copy = nc.vector.tensor_copy if 2 * b in [] else nc.scalar.copy
+            copy(
+                out=x_group(c)[:, :, 128 * r : 128 * r + 128, :].bitcast(F32),
+                in_=live[("xb", b)][:].rearrange("p v z k -> p z k v"),
+            )
+
+        def x_quantise(c, lo, hi):
+            if lo == 0:
                 codes = two.tile([P, 2, TOK], U32, name="x_codes", align_bytes=64)
                 scales = two.tile([P, 2, TOK], U8, name="x_scales", align_bytes=64)
                 live[("xq", c)] = (codes, scales)
-                for z in range(2):
-                    quantise(codes[:, z, :], scales[:, z, :], live[("xg", c)][:, z, :, :])
+            codes, scales = live[("xq", c)]
+            for z in range(2):
+                quantise(codes[:, z, lo:hi], scales[:, z, lo:hi], live[("xg", c)][:, z, lo:hi, :])
 
-        def mx_group(key, lhs, lhs_cols, rhs, rhs_cols):
-            acc = ps_acc.tile([P, 512], F32, name="acc")
-            live[key] = acc
+        def mx_group(acc, lhs, lhs_cols, rhs, rhs_cols):
             for g in range(2):
                 nc.tensor.matmul_mx(
-                    out=acc[:],
+                    out=acc,
                     lhsT=lhs[0][:, g, lhs_cols].bitcast(FP8X4),
                     lhsT_scale=lhs[1][:, g, lhs_cols],
                     rhs=rhs[0][:, g, rhs_cols].bitcast(FP8X4),
@@ -182,30 +236,55 @@ def tile_samplequerymessagepassing_pa_kernel(
                     stop=(g == 1),
                 )
 
+        def parts(i):
+            if i < 4:
+                return [(2 * (i % 2) + j, i // 2, slice(256 * j, 256 * j + 256)) for j in range(2)]
+            return [(i % 8, None, slice(0, 512))]
+
         def layer1(i):
-            if 0 <= i < GROUPS:
-                c, m = i // 8, i % 8
-                mx_group(("a1", i), (w_codes[0], w_scales[0]), slice(m * P, (m + 1) * P), live[("xq", c)], slice(0, TOK))
+            if 0 <= i < STEPS:
+                acc = ps_acc.tile([P, 512], F32, name="acc")
+                live[("a1", i)] = acc
+                for m, half, cols in parts(i):
+                    tok = slice(0, TOK) if half is None else slice(256 * half, 256 * half + 256)
+                    mx_group(acc[:, cols], (w_codes[0], w_scales[0]), slice(m * P, (m + 1) * P), live[("xq", i // 8)], tok)
 
         def gelu1(i):
-            if 0 <= i < GROUPS:
-                c, m = i // 8, i % 8
-                if m == 0:
+            if 0 <= i < STEPS:
+                c = i // 8
+                if i % 8 == 0:
                     h_t = two.tile([P, 8, TOK], BF16, name="h_t")
                     live[("hT", c)] = h_t
-                nc.scalar.activation(
-                    out=live[("hT", c)][:, m, :], in_=live[("a1", i)][:], func=GELU, bias=b0_col[:, m : m + 1], scale=1.0
-                )
+                for m, half, cols in parts(i):
+                    dst, src = live[("hT", c)][:, m, :], live[("a1", i)][:, cols]
+                    if c == 0:
+                        dst = dst.rearrange("p (r h q) -> p h r q", r=4, h=2)
+                        if half is None:
+                            src = src.rearrange("p (h r q) -> p h r q", r=4, h=2)
+                        else:
+                            dst, src = dst[:, half, :, :], src.rearrange("p (r q) -> p r q", r=4)
+                    nc.scalar.activation(out=dst, in_=src, func=GELU, bias=b0_col[:, m : m + 1], scale=1.0)
 
         def h_regroup(i):
-            if 0 <= i < GROUPS and i % 4 == 3:
+            if 0 <= i < STEPS and i % 4 == 3:
                 c, g = i // 8, (i % 8) // 4
                 grouped = two.tile([P, TOK, 4], BF16, name="h_grouped", align_bytes=64)
                 live[("hg", c, g)] = grouped
-                regroup(grouped[:], live[("hT", c)][:, 4 * g : 4 * g + 4, :])
+                if i in []:
+                    for n0 in range(0, TOK, 128):
+                        nc.gpsimd.tensor_scalar(
+                            out=grouped[:, n0 : n0 + 128, :].rearrange("p (c i) t -> p c t i", i=4),
+                            in0=live[("hT", c)][:, 4 * g : 4 * g + 4, n0 : n0 + 128].rearrange("p t (c i) -> p c t i", i=4),
+                            scalar1=1.0,
+                            scalar2=0.0,
+                            op0=MULT,
+                            op1=ADD,
+                        )
+                else:
+                    regroup(nc.scalar.copy if i in [] else nc.vector.tensor_copy, grouped[:], live[("hT", c)][:, 4 * g : 4 * g + 4, :])
 
         def h_quantise(i):
-            if 0 <= i < GROUPS and i % 4 == 3:
+            if 0 <= i < STEPS and i % 4 == 3:
                 c, g = i // 8, (i % 8) // 4
                 if g == 0:
                     codes = three.tile([P, 2, TOK], U32, name="h_codes", align_bytes=64)
@@ -215,58 +294,137 @@ def tile_samplequerymessagepassing_pa_kernel(
                 quantise(codes[:, g, :], scales[:, g, :], live[("hg", c, g)][:])
 
         def layer2(i):
-            if 0 <= i < GROUPS:
+            if 0 <= i < STEPS:
                 c, r, nh = i // 8, (i % 8) // 2, i % 2
-                mx_group(
-                    ("a2", i), live[("hq", c)], slice(r * P, (r + 1) * P),
-                    (w_codes[1], w_scales[1]), slice(nh * 512, (nh + 1) * 512),
-                )
+                acc = ps_acc.tile([P, 512], F32, name="acc")
+                live[("a2", i)] = acc
+                mx_group(acc[:], live[("hq", c)], slice(r * P, (r + 1) * P), (w_codes[1], w_scales[1]), slice(nh * 512, (nh + 1) * 512))
+
+        def spans(i):
+            return [slice(0, 256), slice(256, 512)] if i == STEPS - 1 else [slice(0, 512)]
 
         def add_b1(i):
-            if 0 <= i < GROUPS:
+            if 0 <= i < STEPS:
                 nh = i % 2
                 biased = four.tile([P, 512], F32, name="biased")
                 live[("t", i)] = biased
-                nc.vector.tensor_tensor(
-                    out=biased[:], in0=live[("a2", i)][:], in1=b1_all[:, nh * 512 : (nh + 1) * 512], op=ADD
-                )
+                for cols in spans(i):
+                    nc.vector.tensor_tensor(
+                        out=biased[:, cols], in0=live[("a2", i)][:, cols],
+                        in1=b1_all[:, nh * 512 + cols.start : nh * 512 + cols.stop], op=ADD
+                    )
 
         def gelu2_store(i):
-            if 0 <= i < GROUPS:
+            if 0 <= i < STEPS:
                 c, r, nh = i // 8, (i % 8) // 2, i % 2
                 if nh == 0:
                     rows = four.tile([P, MID], F32, name="rows")
                     live[("o", i // 2)] = rows
                 rows = live[("o", i // 2)]
-                cols = slice(nh * 512, (nh + 1) * 512)
-                nc.scalar.activation(out=rows[:, cols], in_=live[("t", i)][:], func=GELU)
-                dram = out[c].rearrange("(r p) n -> p r n", r=4)
-                if i >= GROUPS - 2:
-                    nc.sync.dma_start(out=dram[:, r, cols], in_=rows[:, cols])
-                elif nh == 1:
+                dram = out[c].rearrange("(r p) n -> p r n" if c in PAIRED else "(p r) n -> p r n", r=4)
+                for span in spans(i):
+                    cols = slice(nh * 512 + span.start, nh * 512 + span.stop)
+                    nc.scalar.activation(out=rows[:, cols], in_=live[("t", i)][:, span], func=GELU)
+                    if i >= STEPS - 2:
+                        nc.sync.dma_start(out=dram[:, r, cols], in_=rows[:, cols])
+                if i < STEPS - 2 and nh == 1:
                     nc.sync.dma_start(out=dram[:, r, :], in_=rows[:])
 
-        def w_slot(k):
-            return 2 * k - 5 if k < 4 else 3 * k - 10
+        def x_bank(b):
+            if b // 4 in PAIRED:
+                x_paired(b)
+                x_paired_copy(b)
+            else:
+                c, r = b // 4, b % 4
+                x_wide(8 * c + 2 * r)
+                x_wide(8 * c + 2 * r + 1)
+
+        def spread_b1():
+            for half in range(2):
+                spread = ps_acc.tile([P, 4, P], F32, name="b1_ps", tag="acc")
+                for m in range(4):
+                    nc.tensor.matmul(
+                        spread[:, m, :],
+                        lhsT=b1_col[:, 4 * half + m : 4 * half + m + 1].to_broadcast([P, P]),
+                        rhs=ident[:],
+                        start=True,
+                        stop=True,
+                    )
+                nc.vector.tensor_copy(out=b1_all[:, 512 * half : 512 * half + 512], in_=spread[:].rearrange("p m n -> p (m n)"))
 
         w_regroup(0)
+        spread_b1()
+        x_wide(0)
+        x_wide(1)
+        x_wide(2)
+        x_wide(3)
         w_regroup(1)
         w_quantise(0)
         w_quantise(1)
-        nc.vector.tensor_copy(out=b0_col[:], in_=bias_ps[:, 0:8])
-        for s in range(-LEAD, GROUPS + LAG + 4):
-            x_matmuls(s + LEAD)
-            layer2(s - LAG)
+        x_quantise(0, 0, 256)
+        layer1(0)
+        w_regroup(2)
+        w_regroup(3)
+        w_quantise(2)
+        w_quantise(3)
+        x_wide(4)
+        x_wide(5)
+        x_wide(6)
+        x_wide(7)
+        gelu1(0)
+        layer1(1)
+        gelu1(1)
+        x_quantise(0, 256, 512)
+        w_regroup(4)
+        w_regroup(5)
+        w_quantise(4)
+        w_quantise(5)
+        layer1(2)
+        layer1(3)
+        gelu1(2)
+        gelu1(3)
+        x_wide(8)
+        x_wide(9)
+        x_wide(10)
+        x_wide(11)
+        w_regroup(6)
+        layer1(4)
+        gelu1(4)
+        layer1(5)
+        gelu1(5)
+        w_regroup(7)
+        w_quantise(6)
+        x_wide(12)
+        layer1(6)
+        gelu1(6)
+        x_wide(13)
+        layer1(7)
+        gelu1(7)
+        x_wide(14)
+        x_wide(15)
+        h_regroup(3)
+        w_quantise(7)
+        h_quantise(3)
+        x_quantise(1, 0, 512)
+        w_regroup(8)
+        w_regroup(9)
+        h_regroup(7)
+        w_quantise(8)
+        w_quantise(9)
+        h_quantise(7)
+        x_bank(8)
+        done = [8]
+        for s in range(8, STEPS + LAG + 3 + 1):
+            for b in range(8, STEPS // 2):
+                if b not in done and s == 2 * b - 8:
+                    x_bank(b)
             layer1(s)
-            x_copy(s + LEAD - 1)
-            gelu2_store(s - LAG - 4)
-            gelu1(s - 1)
-            x_quantise(s + LEAD - 2)
+            layer2(s - LAG)
+            gelu1(s - 1 if s > 8 else -1)
+            gelu2_store(s - LAG - 3)
+            for c in range(2, CHUNKS):
+                if s == 8 * c - 1:
+                    x_quantise(c, 0, 512)
+            h_regroup(s - 2 if s > 9 else -1)
             add_b1(s - LAG - 1)
-            h_regroup(s - 2)
-            h_quantise(s - 4)
-            for k in range(2, 8):
-                if s == w_slot(k):
-                    w_regroup(k)
-                if s == w_slot(k) + 1:
-                    w_quantise(k)
+            h_quantise(s - 2 - 2 if s > 11 else -1)

@@ -151,7 +151,7 @@ def tile_samplequerymessagepassing_pa_kernel(
                         op1=ADD,
                     )
             else:
-                regroup(nc.scalar.copy if k in [3] else nc.vector.tensor_copy, grouped[:, 0:width, :], src)
+                regroup(nc.scalar.copy if k in [] else nc.vector.tensor_copy, grouped[:, 0:width, :], src)
 
         def w_quantise(k):
             layer, g, col, width = W_PIECES[k]
@@ -184,7 +184,7 @@ def tile_samplequerymessagepassing_pa_kernel(
                         stop=True,
                     )
             col = 256 * h + 64 * r if c == 0 else 128 * r + 64 * h
-            copy = nc.vector.tensor_copy if u in [] else nc.scalar.copy
+            copy = nc.vector.tensor_copy if u in [5,7] else nc.scalar.copy
             copy(out=x_group(c)[:, :, col : col + 64, :], in_=bank[:].rearrange("p t z k -> p z k t"))
             if u % 4 == 3:
                 x_late(c, h)
@@ -209,7 +209,7 @@ def tile_samplequerymessagepassing_pa_kernel(
 
         def x_paired_copy(b):
             c, r = b // 4, b % 4
-            copy = nc.vector.tensor_copy if 2 * b in [] else nc.scalar.copy
+            copy = nc.vector.tensor_copy if 2 * b in [5,7] else nc.scalar.copy
             copy(
                 out=x_group(c)[:, :, 128 * r : 128 * r + 128, :].bitcast(F32),
                 in_=live[("xb", b)][:].rearrange("p v z k -> p z k v"),
@@ -333,7 +333,6 @@ def tile_samplequerymessagepassing_pa_kernel(
         def x_bank(b):
             if b // 4 in PAIRED:
                 x_paired(b)
-                x_paired_copy(b)
             else:
                 c, r = b // 4, b % 4
                 x_wide(8 * c + 2 * r)
@@ -412,16 +411,17 @@ def tile_samplequerymessagepassing_pa_kernel(
         w_quantise(8)
         w_quantise(9)
         h_quantise(7)
-        x_bank(8)
-        done = [8]
         for s in range(8, STEPS + LAG + 3 + 1):
             for b in range(8, STEPS // 2):
-                if b not in done and s == 2 * b - 8:
+                if s == max(2 * b - 10, 8):
                     x_bank(b)
             layer1(s)
             layer2(s - LAG)
             gelu1(s - 1 if s > 8 else -1)
             gelu2_store(s - LAG - 3)
+            for b in range(8, STEPS // 2):
+                if s == max(2 * b - 10, 8) + 1:
+                    x_paired_copy(b)
             for c in range(2, CHUNKS):
                 if s == 8 * c - 1:
                     x_quantise(c, 0, 512)

@@ -75,8 +75,8 @@ def tile_samplequerymessagepassing_pa_kernel(
 
         w0_raw = [const.tile([P, 4, W_PIECES[k][3]], BF16, name="w0_raw%d" % k) for k in range(6)]
         w1_raw = [const.tile([P, 4, MID], BF16, name="w1_raw%d" % g) for g in range(2)]
-        w_codes = [const.tile([P, 2, MID], U32, name="w_codes%d" % i, align_bytes=64) for i in range(2)]
-        w_scales = [const.tile([P, 2, MID], U8, name="w_scales%d" % i, align_bytes=64) for i in range(2)]
+        w_codes = [const.tile([P, 2, MID], U32, name="w_codes%d" % i, align_bytes=256) for i in range(2)]
+        w_scales = [const.tile([P, 2, MID], U8, name="w_scales%d" % i, align_bytes=256) for i in range(2)]
         live = {}
 
         def load_x(c, h):
@@ -217,8 +217,8 @@ def tile_samplequerymessagepassing_pa_kernel(
 
         def x_quantise(c, lo, hi):
             if lo == 0:
-                codes = two.tile([P, 2, TOK], U32, name="x_codes", align_bytes=64)
-                scales = two.tile([P, 2, TOK], U8, name="x_scales", align_bytes=64)
+                codes = two.tile([P, 2, TOK], U32, name="x_codes", align_bytes=256)
+                scales = two.tile([P, 2, TOK], U8, name="x_scales", align_bytes=256)
                 live[("xq", c)] = (codes, scales)
             codes, scales = live[("xq", c)]
             for z in range(2):
@@ -287,8 +287,8 @@ def tile_samplequerymessagepassing_pa_kernel(
             if 0 <= i < STEPS and i % 4 == 3:
                 c, g = i // 8, (i % 8) // 4
                 if g == 0:
-                    codes = three.tile([P, 2, TOK], U32, name="h_codes", align_bytes=64)
-                    scales = three.tile([P, 2, TOK], U8, name="h_scales", align_bytes=64)
+                    codes = three.tile([P, 2, TOK], U32, name="h_codes", align_bytes=256)
+                    scales = three.tile([P, 2, TOK], U8, name="h_scales", align_bytes=256)
                     live[("hq", c)] = (codes, scales)
                 codes, scales = live[("hq", c)]
                 quantise(codes[:, g, :], scales[:, g, :], live[("hg", c, g)][:])

from contextlib import ExitStack

import concourse.mybir as mybir
from concourse.masks import make_identity

F32 = mybir.dt.float32
BF16 = mybir.dt.bfloat16
I32 = mybir.dt.int32
U32 = mybir.dt.uint32
U8 = mybir.dt.uint8
FP8X4 = mybir.dt.float8_e4m3fn_x4
GELU = mybir.ActivationFunctionType.Gelu_apprx_tanh
ADD = mybir.AluOpType.add
SUB = mybir.AluOpType.subtract
MULT = mybir.AluOpType.mult

P = 128
CHUNKS = 4
TOK = 512
C = 512
MID = 1024
FLOPS = 2 * (CHUNKS * TOK) * (2 * C) * MID + 2 * (CHUNKS * TOK) * MID * MID

STEPS = 8 * CHUNKS
LAG = 13
PAIRED = [2,3]
W_PIECES = [(0, 0, 0, 256), (0, 1, 0, 256), (0, 0, 256, 256), (0, 1, 256, 256), (0, 0, 512, 512), (0, 1, 512, 512), (1, 0, 0, 512), (1, 0, 512, 512), (1, 1, 0, 512), (1, 1, 512, 512)]


def block(t):
    return 2 * (t % 2) + t // 2


def tile_samplequerymessagepassing_pa_kernel(
    tc, sample_features, query_samples, pos_enc, W0, b0, W1, b1, out
):
    nc = tc.nc
    with ExitStack() as ctx:
        const = ctx.enter_context(tc.tile_pool(name="const", bufs=1))
        two = ctx.enter_context(tc.tile_pool(name="two", bufs=2))
        three = ctx.enter_context(tc.tile_pool(name="three", bufs=3))
        four = ctx.enter_context(tc.tile_pool(name="four", bufs=4))
        ps_acc = ctx.enter_context(tc.psum_pool(name="ps_acc", bufs=5))
        ps_x = ctx.enter_context(tc.psum_pool(name="ps_x", bufs=3))
        ctx.enter_context(tc.manual_schedule())

        zero = const.tile([P, 1], F32, name="zero")
        nc.vector.memset(zero[:], 0.0)
        brow = const.tile([P, P], BF16, name="brow")
        nc.vector.memset(brow[:], 0.0)
        nc.scalar.dma_start(out=brow[0:8, :], in_=b0.rearrange("(m p) -> m p", p=P))
        nc.scalar.dma_start(out=brow[8:16, :], in_=b1.rearrange("(m p) -> m p", p=P))
        stacked = [[const.tile([P, 2, 4, C], BF16, name="stacked%d%d" % (i, h)) for h in range(2)] for i in range(2)]

        def zero_v(t):
            nc.vector.memset(t[:].bitcast(I32), 0)

        def zero_s(t):
            nc.scalar.copy(out=t[:].rearrange("p a r ch -> p (a r ch)").bitcast(F32), in_=zero[:].to_broadcast([P, 4 * C]))

        zero_v(stacked[0][0])
        zero_v(stacked[0][1])
        nc.scalar.activation(out=zero[:], in_=zero[:], func=GELU)
        zero_s(stacked[1][0])
        ident = const.tile([P, P], BF16, name="ident")
        make_identity(nc, ident[:])
        sel = const.tile([P, 2, 32], BF16, name="sel")
        by_slot = ident[:].rearrange("p (j s) -> p j s", s=4)
        nc.gpsimd.tensor_tensor(out=sel[:, 1, :], in0=by_slot[:, :, 1], in1=by_slot[:, :, 2], op=ADD)
        nc.gpsimd.tensor_tensor(out=sel[:, 0, :], in0=by_slot[:, :, 0], in1=sel[:, 1, :], op=SUB)
        nc.gpsimd.memset(stacked[1][1][:].bitcast(I32), 0)
        b0_col = const.tile([P, 8], F32, name="b0_col")
        b1_col = const.tile([P, 8], BF16, name="b1_col")
        b1_all = const.tile([P, MID], BF16, name="b1_all")

        w0_raw = [const.tile([P, 4, W_PIECES[k][3]], BF16, name="w0_raw%d" % k) for k in range(6)]
        w1_raw = [const.tile([P, 4, MID], BF16, name="w1_raw%d" % g) for g in range(2)]
        w_codes = [const.tile([P, 2, MID], U32, name="w_codes%d" % i, align_bytes=256) for i in range(2)]
        w_scales = [const.tile([P, 2, MID], U8, name="w_scales%d" % i, align_bytes=256) for i in range(2)]
        live = {}

        def load_x(c, h):
            for s, src in enumerate((sample_features, query_samples, pos_enc)):
                dst = stacked[c % 2][h][s:P:4, :, :, :]
                if c in PAIRED:
                    view = src[c].rearrange("(h g j) (u ch) -> (j u) h g ch", h=2, g=16, u=2)
                    nc.sync.dma_start(out=dst.rearrange("p a r (q ch) -> p (a r q) ch", q=2), in_=view[:, h, :, :])
                else:
                    view = src[c].rearrange("(a j r) ch -> j a (r ch)", a=4, r=4)
                    nc.sync.dma_start(out=dst.rearrange("p a r ch -> p a (r ch)"), in_=view[:, 2 * h : 2 * h + 2, :])

        def load_w0(k):
            layer, g, col, width = W_PIECES[k]
            rows = W0[g * 512 : (g + 1) * 512, col : col + width].rearrange("(u v p) n -> p v u n", v=2, p=P)
            for v in range(2):
                nc.sync.dma_start(out=w0_raw[k][:, 2 * v : 2 * v + 2, :], in_=rows[:, v, :, :])

        def load(name):
            if name[0] == "w":
                load_w0(int(name[1]))
            elif name[0] == "v":
                g = int(name[1])
                nc.sync.dma_start(out=w1_raw[g][:], in_=W1[g * 512 : (g + 1) * 512, :].rearrange("(t p) n -> p t n", p=P))
            else:
                load_x(int(name[1]), int(name[2]))

        for name in ["w0","x00","w1","w2","w3","x01","w4","w5","x10","v0","x11","v1"]:
            load(name)
        bias_ps = ps_acc.tile([P, P], BF16, name="bias_ps", tag="acc")
        nc.tensor.transpose(bias_ps[:], brow[:], ident[:])
        nc.vector.tensor_copy(out=b0_col[:], in_=bias_ps[:, 0:8])
        nc.vector.tensor_copy(out=b1_col[:], in_=bias_ps[:, 8:16])

        def regroup(copy, dst, src):
            copy(out=dst.rearrange("p (c i) t -> p c t i", i=4), in_=src.rearrange("p t (c i) -> p c t i", i=4))

        def quantise(codes, scales, grouped):
            nc.vector.quantize_mx(out=codes.bitcast(FP8X4), scales=scales, in_=grouped.rearrange("p n t -> p (n t)"))

        def w_source(k):
            layer, g, col, width = W_PIECES[k]
            return w0_raw[k][:] if layer == 0 else w1_raw[g][:, :, col : col + width]

        def w_regroup(k):
            width = W_PIECES[k][3]
            grouped = three.tile([P, 512, 4], BF16, name="w_grouped", align_bytes=64)
            live[("wg", k)] = grouped
            src = w_source(k)
            if k in [5,8]:
                for n0 in range(0, width, 256):
                    bank = ps_acc.tile([P, 512], F32, name="w_bank", tag="acc")
                    for q in range(2):
                        n1 = n0 + 128 * q
                        nc.tensor.matmul(
                            bank[:].bitcast(BF16)[:, 512 * q : 512 * q + 512],
                            lhsT=ident[:],
                            rhs=src[:, :, n1 : n1 + 128].rearrange("p t n -> p n t"),
                            start=True,
                            stop=True,
                        )
                    copy = nc.vector.tensor_copy if k in [] else nc.scalar.copy
                    copy(out=grouped[:, n0 : n0 + 256, :].rearrange("p n t -> p (n t)").bitcast(F32), in_=bank[:])
            elif k in []:
                for n0 in range(0, width, 128):
                    nc.gpsimd.tensor_scalar(
                        out=grouped[:, n0 : n0 + 128, :].rearrange("p (c i) t -> p c t i", i=4),
                        in0=src[:, :, n0 : n0 + 128].rearrange("p t (c i) -> p c t i", i=4),
                        scalar1=1.0,
                        scalar2=0.0,
                        op0=MULT,
                        op1=ADD,
                    )
            else:
                regroup(nc.scalar.copy if k in [] else nc.vector.tensor_copy, grouped[:, 0:width, :], src)

        def w_quantise(k):
            layer, g, col, width = W_PIECES[k]
            cols = slice(col, col + width)
            quantise(w_codes[layer][:, g, cols], w_scales[layer][:, g, cols], live[("wg", k)][:, 0:width, :])

        def x_group(c):
            if ("xg", c) not in live:
                x_grouped = two.tile([P, 2, TOK, 4], BF16, name="x_grouped", align_bytes=64)
                live[("xg", c)] = x_grouped
            return live[("xg", c)]

        def x_late(c, h):
            if c + 2 < CHUNKS:
                load_x(c + 2, h)
                if (c, h) == (0, 1):
                    for name in []:
                        load(name)

        def x_wide(u):
            c, h, r = u // 8, (u % 8) // 4, u % 4
            bank = ps_x.tile([P, 4, 2, 64], F32, name="x_bank")
            for a in range(2):
                for t in range(4):
                    nc.tensor.matmul(
                        bank[:, t, :, 32 * a : 32 * a + 32],
                        lhsT=stacked[c % 2][h][:, a, r, block(t) * P : (block(t) + 1) * P],
                        rhs=sel[:],
                        start=True,
                        stop=True,
                    )
            col = 256 * h + 64 * r if c == 0 else 128 * r + 64 * h
            copy = nc.vector.tensor_copy if u in [5,7] else nc.scalar.copy
            copy(out=x_group(c)[:, :, col : col + 64, :], in_=bank[:].rearrange("p t z k -> p z k t"))
            if u % 4 == 3:
                x_late(c, h)

        def x_paired(b):
            c, r = b // 4, b % 4
            bank = ps_x.tile([P, 2, 2, P], F32, name="x_bank")
            pairs = bank[:].bitcast(BF16)
            rows = stacked[c % 2][r // 2][:].rearrange("p a r (q ch) -> p (a r q) ch", q=2)
            for v in range(2):
                for i in range(8):
                    nc.tensor.matmul(
                        pairs[:, v, :, 32 * i : 32 * i + 32],
                        lhsT=rows[:, 8 * (r % 2) + i, v * P : (v + 1) * P],
                        rhs=sel[:],
                        start=True,
                        stop=True,
                    )
            live[("xb", b)] = bank
            if r % 2 == 1:
                x_late(c, r // 2)

        def x_paired_copy(b):
            c, r = b // 4, b % 4
            copy = nc.vector.tensor_copy if 2 * b in [5,7] else nc.scalar.copy
            copy(
                out=x_group(c)[:, :, 128 * r : 128 * r + 128, :].bitcast(F32),
                in_=live[("xb", b)][:].rearrange("p v z k -> p z k v"),
            )

        def x_quantise(c, lo, hi):
            if lo == 0:
                codes = two.tile([P, 2, TOK], U32, name="x_codes", align_bytes=256)
                scales = two.tile([P, 2, TOK], U8, name="x_scales", align_bytes=256)
                live[("xq", c)] = (codes, scales)
            codes, scales = live[("xq", c)]
            for z in range(2):
                quantise(codes[:, z, lo:hi], scales[:, z, lo:hi], live[("xg", c)][:, z, lo:hi, :])

        def mx_group(acc, lhs, lhs_cols, rhs, rhs_cols):
            for g in range(2):
                nc.tensor.matmul_mx(
                    out=acc,
                    lhsT=lhs[0][:, g, lhs_cols].bitcast(FP8X4),
                    lhsT_scale=lhs[1][:, g, lhs_cols],
                    rhs=rhs[0][:, g, rhs_cols].bitcast(FP8X4),
                    rhs_scale=rhs[1][:, g, rhs_cols],
                    start=(g == 0),
                    stop=(g == 1),
                )

        def parts(i):
            if i < 4:
                return [(2 * (i % 2) + j, i // 2, slice(256 * j, 256 * j + 256)) for j in range(2)]
            return [(i % 8, None, slice(0, 512))]

        def layer1(i):
            if 0 <= i < STEPS:
                acc = ps_acc.tile([P, 512], F32, name="acc")
                live[("a1", i)] = acc
                for m, half, cols in parts(i):
                    tok = slice(0, TOK) if half is None else slice(256 * half, 256 * half + 256)
                    mx_group(acc[:, cols], (w_codes[0], w_scales[0]), slice(m * P, (m + 1) * P), live[("xq", i // 8)], tok)

        def gelu1(i):
            if 0 <= i < STEPS:
                c = i // 8
                if i % 8 == 0:
                    h_t = two.tile([P, 8, TOK], BF16, name="h_t")
                    live[("hT", c)] = h_t
                for m, half, cols in parts(i):
                    dst, src = live[("hT", c)][:, m, :], live[("a1", i)][:, cols]
                    if c == 0:
                        dst = dst.rearrange("p (r h q) -> p h r q", r=4, h=2)
                        if half is None:
                            src = src.rearrange("p (h r q) -> p h r q", r=4, h=2)
                        else:
                            dst, src = dst[:, half, :, :], src.rearrange("p (r q) -> p r q", r=4)
                    nc.scalar.activation(out=dst, in_=src, func=GELU, bias=b0_col[:, m : m + 1], scale=1.0)

        def h_regroup(i):
            if 0 <= i < STEPS and i % 4 == 3:
                c, g = i // 8, (i % 8) // 4
                grouped = two.tile([P, TOK, 4], BF16, name="h_grouped", align_bytes=64)
                live[("hg", c, g)] = grouped
                if i in []:
                    for n0 in range(0, TOK, 128):
                        nc.gpsimd.tensor_scalar(
                            out=grouped[:, n0 : n0 + 128, :].rearrange("p (c i) t -> p c t i", i=4),
                            in0=live[("hT", c)][:, 4 * g : 4 * g + 4, n0 : n0 + 128].rearrange("p t (c i) -> p c t i", i=4),
                            scalar1=1.0,
                            scalar2=0.0,
                            op0=MULT,
                            op1=ADD,
                        )
                else:
                    regroup(nc.scalar.copy if i in [] else nc.vector.tensor_copy, grouped[:], live[("hT", c)][:, 4 * g : 4 * g + 4, :])

        def h_quantise(i):
            if 0 <= i < STEPS and i % 4 == 3:
                c, g = i // 8, (i % 8) // 4
                if g == 0:
                    codes = three.tile([P, 2, TOK], U32, name="h_codes", align_bytes=256)
                    scales = three.tile([P, 2, TOK], U8, name="h_scales", align_bytes=256)
                    live[("hq", c)] = (codes, scales)
                codes, scales = live[("hq", c)]
                quantise(codes[:, g, :], scales[:, g, :], live[("hg", c, g)][:])

        def layer2(i):
            if 0 <= i < STEPS:
                c, r, nh = i // 8, (i % 8) // 2, i % 2
                acc = ps_acc.tile([P, 512], F32, name="acc")
                live[("a2", i)] = acc
                mx_group(acc[:], live[("hq", c)], slice(r * P, (r + 1) * P), (w_codes[1], w_scales[1]), slice(nh * 512, (nh + 1) * 512))

        def spans(i):
            return [slice(0, 256), slice(256, 512)] if i == STEPS - 1 else [slice(0, 512)]

        def add_b1(i):
            if 0 <= i < STEPS:
                nh = i % 2
                biased = four.tile([P, 512], F32, name="biased")
                live[("t", i)] = biased
                for cols in spans(i):
                    nc.vector.tensor_tensor(
                        out=biased[:, cols], in0=live[("a2", i)][:, cols],
                        in1=b1_all[:, nh * 512 + cols.start : nh * 512 + cols.stop], op=ADD
                    )

        def gelu2_store(i):
            if 0 <= i < STEPS:
                c, r, nh = i // 8, (i % 8) // 2, i % 2
                if nh == 0:
                    rows = four.tile([P, MID], F32, name="rows")
                    live[("o", i // 2)] = rows
                rows = live[("o", i // 2)]
                dram = out[c].rearrange("(r p) n -> p r n" if c in PAIRED else "(p r) n -> p r n", r=4)
                for span in spans(i):
                    cols = slice(nh * 512 + span.start, nh * 512 + span.stop)
                    nc.scalar.activation(out=rows[:, cols], in_=live[("t", i)][:, span], func=GELU)
                    if i >= STEPS - 2:
                        nc.sync.dma_start(out=dram[:, r, cols], in_=rows[:, cols])
                if i < STEPS - 2 and nh == 1:
                    nc.sync.dma_start(out=dram[:, r, :], in_=rows[:])

        def x_bank(b):
            if b // 4 in PAIRED:
                x_paired(b)
            else:
                c, r = b // 4, b % 4
                x_wide(8 * c + 2 * r)
                x_wide(8 * c + 2 * r + 1)

        def spread_b1():
            for half in range(2):
                spread = ps_acc.tile([P, 4, P], F32, name="b1_ps", tag="acc")
                for m in range(4):
                    nc.tensor.matmul(
                        spread[:, m, :],
                        lhsT=b1_col[:, 4 * half + m : 4 * half + m + 1].to_broadcast([P, P]),
                        rhs=ident[:],
                        start=True,
                        stop=True,
                    )
                nc.vector.tensor_copy(out=b1_all[:, 512 * half : 512 * half + 512], in_=spread[:].rearrange("p m n -> p (m n)"))

        w_regroup(0)
        spread_b1()
        x_wide(0)
        x_wide(1)
        x_wide(2)
        x_wide(3)
        w_regroup(1)
        w_quantise(0)
        w_quantise(1)
        x_quantise(0, 0, 256)
        layer1(0)
        w_regroup(2)
        w_regroup(3)
        w_quantise(2)
        w_quantise(3)
        x_wide(4)
        x_wide(5)
        x_wide(6)
        x_wide(7)
        gelu1(0)
        layer1(1)
        gelu1(1)
        x_quantise(0, 256, 512)
        w_regroup(4)
        w_regroup(5)
        w_quantise(4)
        w_quantise(5)
        layer1(2)
        layer1(3)
        gelu1(2)
        gelu1(3)
        x_wide(8)
        x_wide(9)
        x_wide(10)
        x_wide(11)
        w_regroup(6)
        layer1(4)
        gelu1(4)
        layer1(5)
        gelu1(5)
        w_regroup(7)
        w_quantise(6)
        x_wide(12)
        layer1(6)
        gelu1(6)
        x_wide(13)
        layer1(7)
        gelu1(7)
        x_wide(14)
        x_wide(15)
        h_regroup(3)
        w_quantise(7)
        h_quantise(3)
        x_quantise(1, 0, 512)
        w_regroup(8)
        w_regroup(9)
        h_regroup(7)
        w_quantise(8)
        w_quantise(9)
        h_quantise(7)
        for s in range(8, STEPS + LAG + 3 + 1):
            for b in range(8, STEPS // 2):
                if s == max(2 * b - 10, 8):
                    x_bank(b)
            layer1(s)
            layer2(s - LAG)
            gelu1(s - 1 if s > 8 else -1)
            gelu2_store(s - LAG - 3)
            for b in range(8, STEPS // 2):
                if s == max(2 * b - 10, 8) + 1:
                    x_paired_copy(b)
            for c in range(2, CHUNKS):
                if s == 8 * c - 1:
                    x_quantise(c, 0, 512)
            h_regroup(s - 2 if s > 9 else -1)
            add_b1(s - LAG - 1)
            h_quantise(s - 2 - 2 if s > 11 else -1)
